import numpy as np
import ml_dtypes


def mxq(x, axis, fmt="e4m3"):
    dtype, down = {"e4m3": (ml_dtypes.float8_e4m3fn, 7), "e5m2": (ml_dtypes.float8_e5m2, 14)}[fmt]
    v = np.moveaxis(np.asarray(x, np.float32).astype(ml_dtypes.bfloat16).astype(np.float64), axis, -1)
    blocks = v.reshape(v.shape[:-1] + (-1, 32))
    amax = np.abs(blocks).max(-1, keepdims=True)
    byte = np.maximum(np.where(amax > 0, np.frexp(amax)[1] - 1 + 127, 0) - down, 1)
    scale = np.exp2(byte - 127.0)
    codes = (blocks / scale).astype(np.float32).astype(dtype).astype(np.float64)
    return np.moveaxis((codes * scale).reshape(v.shape), -1, axis)


WIDE = False


def mx_kscale(k):
    if not WIDE:
        return np.ones(k)
    levels = np.array([10, -10, 5, -5, 0])
    a = np.random.permutation(np.resize(levels, k // 512 * 4)).reshape(k // 512, 4)
    idx = np.arange(k)
    return np.exp2(a[idx // 512, idx % 128 // 32])


BF16 = ml_dtypes.bfloat16


def bf(x):
    return np.asarray(x, np.float32).astype(BF16)


def f64(x):
    return np.asarray(x).astype(np.float64)


N, F, H = 1536, 512, 512
SIG = 1.5


def elu(v):
    return np.where(v > 0.0, v, np.exp(np.minimum(v, 0.0)) - 1.0)


def log_softmax(v):
    z = v - v.max(axis=1, keepdims=True)
    return z - np.log(np.exp(z).sum(axis=1, keepdims=True))


def draw_adj():
    r = np.random.uniform(0.5, 1.5, (N, 1))
    return 2.0 * r * np.exp(SIG * np.random.standard_normal((N, N)) - 0.5 * SIG * SIG) / N


def setup_inputs():
    s = mx_kscale(H)
    x = elu(np.random.standard_normal((N, H)) * 0.9 + np.random.standard_normal(H) * 0.9)
    return {"x_gc2": bf(x * s),
            "adj1": bf(draw_adj()),
            "W3": bf(np.random.standard_normal((2 * H, H)) / np.sqrt(2 * H) / np.tile(s, 2)[:, None]),
            "b3": bf(np.random.standard_normal(H) * 0.3)}


def reference(x_gc2, adj1, W3, b3):
    xq = mxq(f64(x_gc2), 1, "e4m3")
    w = f64(W3)
    a = f64(adj1)
    top = xq @ mxq(w[:H], 0, "e4m3")
    bot = xq @ mxq(w[H:], 0, "e4m3")
    deg = a.sum(axis=1, keepdims=True)
    y = top * deg + (mxq(a, 1, "e4m3") @ mxq(bot, 0, "e4m3")) + f64(b3)
    return log_softmax(y)

@@ -1,0 +1,265 @@
+from contextlib import ExitStack
+
+import concourse.mybir as mybir
+from concourse.masks import make_identity
+
+FLOPS = 2 * 1536 * 512 * 512 * 2 + 2 * 1536 * 1536 * 512
+
+F32 = mybir.dt.float32
+BF16 = mybir.dt.bfloat16
+U32 = mybir.dt.uint32
+U8 = mybir.dt.uint8
+FP8X4 = mybir.dt.float8_e4m3fn_x4
+ALU = mybir.AluOpType
+ACT = mybir.ActivationFunctionType
+AX = mybir.AxisListType
+
+P = 128
+H = 512
+NODES = 1536
+NG = 3
+NPAIR = 6
+NT = 12
+
+DEG_ON_VECTOR = (0, 2, 3, 5, 6, 8, 9, 11)
+LN_GROUPS = ((0, 8), (8, 12))
+BOT_EVAC_ON_VECTOR = (1, 3)
+
+
+def tile_gcn_pc_kernel(tc, x_gc2, adj1, W3, b3, out):
+    nc = tc.nc
+    with ExitStack() as ctx:
+        keep = ctx.enter_context(tc.tile_pool(name="keep", bufs=1))
+        grp_pool = ctx.enter_context(tc.tile_pool(name="grp", bufs=6))
+        work = ctx.enter_context(tc.tile_pool(name="work", bufs=3))
+        junk = ctx.enter_context(tc.tile_pool(name="junk", bufs=2))
+        ps_tr = ctx.enter_context(tc.psum_pool(name="pstr", bufs=3))
+        ps_acc = ctx.enter_context(tc.psum_pool(name="psacc", bufs=5))
+
+        x_v = x_gc2.rearrange("(a m e) k -> m a (e k)", a=NPAIR, m=P, e=2)
+        adj_v = adj1.rearrange("(a m e) j -> m a (e j)", a=NPAIR, m=P, e=2)
+        w_v = W3.rearrange("(w h q e) c -> q w h (e c)", w=2, h=2, q=P, e=2)
+        out_v = out.rearrange("(a m e) c -> m a (e c)", a=NPAIR, m=P, e=2)
+
+        w_raw = [keep.tile([P, 4 * H], BF16, name="w_raw%d" % w) for w in range(2)]
+        w_grp = [keep.tile([P, 4 * H], BF16, name="w_grp%d" % w, align_bytes=64) for w in range(2)]
+        wq = [keep.tile([P, H], U32, name="wq%d" % w, align_bytes=64) for w in range(2)]
+        ws = [keep.tile([P, H], U8, name="ws%d" % w, align_bytes=64) for w in range(2)]
+        x_sb = [keep.tile([P, 4 * H], BF16, name="x_sb%d" % g) for g in range(NG)]
+        x_grp = [keep.tile([P, 4 * H], BF16, name="x_grp%d" % g, align_bytes=64) for g in range(NG)]
+        xq = [keep.tile([P, H], U32, name="xq%d" % g, align_bytes=64) for g in range(NG)]
+        xs = [keep.tile([P, H], U8, name="xs%d" % g, align_bytes=64) for g in range(NG)]
+        bot_grp = [keep.tile([P, 4 * H], BF16, name="bot_grp%d" % g, align_bytes=64) for g in range(NG)]
+        botq = [keep.tile([P, H], U32, name="botq%d" % g, align_bytes=64) for g in range(NG)]
+        bots = [keep.tile([P, H], U8, name="bots%d" % g, align_bytes=64) for g in range(NG)]
+        adj_sb = [keep.tile([P, 2 * NODES], BF16, name="adj_sb%d" % a) for a in range(NPAIR)]
+        adjq = [keep.tile([P, NG * 256], U32, name="adjq%d" % a, align_bytes=64) for a in range(NPAIR)]
+        adjs = [keep.tile([P, NG * 256], U8, name="adjs%d" % a, align_bytes=64) for a in range(NPAIR)]
+        y_sb = [keep.tile([P, 2 * H], F32, name="y_sb%d" % a) for a in range(NPAIR)]
+        deg = [keep.tile([P, 1], F32, name="deg%d" % n) for n in range(NT)]
+        negm = keep.tile([P, NT], F32, name="negm")
+        sums = keep.tile([P, NT], F32, name="sums")
+        lns = keep.tile([P, NT], F32, name="lns")
+        shift = keep.tile([P, NT], F32, name="shift")
+        ident = keep.tile([P, P], F32, name="ident")
+        ones = keep.tile([P, P], BF16, name="ones")
+        b3row = keep.tile([P, H], BF16, name="b3row")
+        b3bc = keep.tile([P, H], F32, name="b3bc")
+        warm = keep.tile([P, 2], F32, name="warm")
+
+        nc.sync.dma_start(out=w_raw[1][:].rearrange("q (h f) -> q h f", h=2), in_=w_v[:, 1])
+        for g in range(NG):
+            nc.sync.dma_start(
+                out=x_sb[g][:].rearrange("m (a f) -> m a f", a=2), in_=x_v[:, 2 * g : 2 * g + 2, :]
+            )
+        nc.sync.dma_start(out=w_raw[0][:].rearrange("q (h f) -> q h f", h=2), in_=w_v[:, 0])
+        for a in range(NPAIR):
+            nc.sync.dma_start(out=adj_sb[a][:], in_=adj_v[:, a, :])
+
+        nc.vector.memset(warm[:], 0.0)
+        nc.scalar.activation(out=warm[:, 1:2], in_=warm[:, 0:1], func=ACT.Exp)
+        make_identity(nc, ident[:])
+        nc.vector.memset(ones[:], 1.0)
+        nc.vector.memset(b3row[:], 0.0)
+        nc.scalar.dma_start(out=b3row[0:1, :], in_=b3.unsqueeze(0))
+
+        def regroup_weights(w):
+            nc.vector.tensor_copy(
+                out=w_grp[w][:].rearrange("p (c i t) -> p c t i", c=P, i=4, t=4),
+                in_=w_raw[w][:].rearrange("p (t c i) -> p c t i", t=4, c=P, i=4),
+            )
+
+        def quantise_weights(w):
+            nc.vector.quantize_mx(out=wq[w][:].bitcast(FP8X4), scales=ws[w][:], in_=w_grp[w][:])
+
+        def x_transposes(g):
+            words = x_sb[g][:].bitcast(F32)
+            grouped = x_grp[g][:].bitcast(F32)
+            for b in range(2):
+                bank = ps_tr.tile([P, H], F32, name="tr")
+                for n2 in range(2):
+                    for h in range(2):
+                        nc.tensor.transpose(
+                            bank[:, (2 * n2 + h) * P : (2 * n2 + h + 1) * P],
+                            words[:, (2 * b + n2) * 256 + h * P : (2 * b + n2) * 256 + (h + 1) * P],
+                            ident[:],
+                        )
+                nc.scalar.copy(
+                    out=grouped[:, b * H : (b + 1) * H].rearrange("q (n r h) -> q n r h", n=2, r=P, h=2),
+                    in_=bank[:].rearrange("q (n h r) -> q n r h", n=2, h=2, r=P),
+                )
+
+        def x_quantise(g):
+            nc.vector.quantize_mx(out=xq[g][:].bitcast(FP8X4), scales=xs[g][:], in_=x_grp[g][:])
+
+        def bot_passes(g):
+            for cs in range(4):
+                bank = ps_acc.tile([P, H], F32, name="acc")
+                for t in range(4):
+                    nc.tensor.matmul_mx(
+                        out=bank[:, t * P : (t + 1) * P],
+                        lhsT=xq[g][:, t * P : (t + 1) * P].bitcast(FP8X4),
+                        lhsT_scale=xs[g][:, t * P : (t + 1) * P],
+                        rhs=wq[1][:, cs * P : (cs + 1) * P].bitcast(FP8X4),
+                        rhs_scale=ws[1][:, cs * P : (cs + 1) * P],
+                        start=True,
+                        stop=True,
+                    )
+                dst = bot_grp[g][:, cs * H : (cs + 1) * H].rearrange("m (c t) -> m c t", c=P, t=4)
+                src = bank[:].rearrange("m (t c) -> m c t", t=4, c=P)
+                if cs in BOT_EVAC_ON_VECTOR:
+                    nc.vector.tensor_copy(out=dst, in_=src)
+                else:
+                    nc.scalar.copy(out=dst, in_=src)
+
+        def bot_quantise(g):
+            nc.vector.quantize_mx(out=botq[g][:].bitcast(FP8X4), scales=bots[g][:], in_=bot_grp[g][:])
+
+        def adj_stage(a):
+            words = adj_sb[a][:].bitcast(F32)
+            grouped = []
+            for g in range(NG):
+                bank = ps_tr.tile([P, H], F32, name="tr")
+                for e in range(2):
+                    for u in range(2):
+                        col = e * 768 + g * 256 + u * P
+                        nc.tensor.transpose(
+                            bank[:, (2 * e + u) * P : (2 * e + u + 1) * P], words[:, col : col + P], ident[:]
+                        )
+                agrp = grp_pool.tile([P, 2 * H], BF16, name="agrp", align_bytes=64)
+                nc.scalar.copy(
+                    out=agrp[:].bitcast(F32).rearrange("q (e i u) -> q e i u", e=2, i=P, u=2),
+                    in_=bank[:].rearrange("q (e u i) -> q e i u", e=2, u=2, i=P),
+                )
+                grouped.append(agrp)
+            for e in range(2):
+                n = 2 * a + e
+                rows = adj_sb[a][:, e * NODES : (e + 1) * NODES]
+                dj = junk.tile([P, NODES], BF16, name="dj")
+                if n in DEG_ON_VECTOR:
+                    nc.vector.tensor_scalar(
+                        out=dj[:], in0=rows, scalar1=1.0, scalar2=None, op0=ALU.mult, op1=ALU.add,
+                        accum_out=deg[n][:],
+                    )
+                else:
+                    nc.scalar.activation(out=dj[:], in_=rows, func=ACT.Copy, accum_out=deg[n][:])
+            for g in range(NG):
+                nc.vector.quantize_mx(
+                    out=adjq[a][:, g * 256 : (g + 1) * 256].bitcast(FP8X4),
+                    scales=adjs[a][:, g * 256 : (g + 1) * 256],
+                    in_=grouped[g][:],
+                )
+
+        def epilogue(a):
+            tops = []
+            abs_ = []
+            for e in range(2):
+                n = 2 * a + e
+                g0, t0 = n // 4, n % 4
+                top_ps = ps_acc.tile([P, H], F32, name="acc")
+                nc.tensor.matmul_mx(
+                    out=top_ps[:],
+                    lhsT=xq[g0][:, t0 * P : (t0 + 1) * P].bitcast(FP8X4),
+                    lhsT_scale=xs[g0][:, t0 * P : (t0 + 1) * P],
+                    rhs=wq[0][:].bitcast(FP8X4),
+                    rhs_scale=ws[0][:],
+                    start=True,
+                    stop=True,
+                )
+                ab_ps = ps_acc.tile([P, H], F32, name="acc")
+                for g in range(NG):
+                    col = g * 256 + e * P
+                    nc.tensor.matmul_mx(
+                        out=ab_ps[:],
+                        lhsT=adjq[a][:, col : col + P].bitcast(FP8X4),
+                        lhsT_scale=adjs[a][:, col : col + P],
+                        rhs=botq[g][:].bitcast(FP8X4),
+                        rhs_scale=bots[g][:],
+                        start=(g == 0),
+                        stop=(g == NG - 1),
+                    )
+                tops.append(top_ps)
+                abs_.append(ab_ps)
+            for e in range(2):
+                n = 2 * a + e
+                y = y_sb[a][:, e * H : (e + 1) * H]
+                t1 = work.tile([P, H], F32, name="t1")
+                nc.vector.scalar_tensor_tensor(
+                    out=t1[:], in0=tops[e][:], scalar=deg[n][:], in1=b3bc[:], op0=ALU.mult, op1=ALU.add
+                )
+                nc.vector.tensor_tensor(out=y, in0=abs_[e][:], in1=t1[:], op=ALU.add)
+                nc.vector.tensor_reduce(out=negm[:, n : n + 1], in_=y, axis=AX.X, op=ALU.max, negate=True)
+                ej = junk.tile([P, H], BF16, name="ej")
+                nc.scalar.activation(
+                    out=ej[:], in_=y, func=ACT.Exp, bias=negm[:, n : n + 1], scale=1.0,
+                    accum_out=sums[:, n : n + 1],
+                )
+
+        def finish(lo, hi, last):
+            nc.scalar.activation(out=lns[:, lo:hi], in_=sums[:, lo:hi], func=ACT.Ln)
+            nc.vector.tensor_tensor(out=shift[:, lo:hi], in0=negm[:, lo:hi], in1=lns[:, lo:hi], op=ALU.subtract)
+            for n in range(lo, hi):
+                a, e = n // 2, n % 2
+                y = y_sb[a][:, e * H : (e + 1) * H]
+                if last and e == 0:
+                    nc.vector.tensor_scalar(
+                        out=y, in0=y, scalar1=shift[:, n : n + 1], scalar2=None, op0=ALU.add
+                    )
+                elif last:
+                    nc.scalar.activation(out=y, in_=y, func=ACT.Identity, bias=shift[:, n : n + 1], scale=1.0)
+                else:
+                    nc.gpsimd.tensor_scalar(
+                        out=y, in0=y, scalar1=1.0, scalar2=shift[:, n : n + 1], op0=ALU.mult, op1=ALU.add
+                    )
+                nc.sync.dma_start(out=out_v[:, a, e * H : (e + 1) * H], in_=y)
+
+        regroup_weights(1)
+        x_transposes(0)
+        quantise_weights(1)
+        x_transposes(1)
+        x_quantise(0)
+        bot_passes(0)
+        x_transposes(2)
+        x_quantise(1)
+        bot_passes(1)
+        x_quantise(2)
+        bot_quantise(0)
+        bot_passes(2)
+        b3_ps = ps_tr.tile([P, H], F32, name="tr")
+        nc.tensor.matmul(out=b3_ps[:], lhsT=ones[:], rhs=b3row[:], start=True, stop=True)
+        nc.scalar.copy(out=b3bc[:], in_=b3_ps[:])
+        regroup_weights(0)
+        bot_quantise(1)
+        adj_stage(0)
+        bot_quantise(2)
+        quantise_weights(0)
+        adj_stage(1)
+        grp = 0
+        for a in range(NPAIR):
+            if a + 2 < NPAIR:
+                adj_stage(a + 2)
+            epilogue(a)
+            lo, hi = LN_GROUPS[grp]
+            if 2 * a + 2 == hi:
+                finish(lo, hi, grp == len(LN_GROUPS) - 1)
+                grp += 1

@@ -20,21 +20,56 @@ NODES = 1536
 NG = 3
 NPAIR = 6
 NT = 12
+RP = 3
+LOADS = (("x", 0), ("w", 1), ("x", 1), ("x", 2), ("w", 0), ("a", 0), ("a", 1), ("a", 2), ("a", 3), ("a", 4), ("a", 5))
 
-DEG_ON_VECTOR = (0, 2, 3, 5, 6, 8, 9, 11)
-LN_GROUPS = ((0, 8), (8, 12))
-BOT_EVAC_ON_VECTOR = (1, 3)
+ORDER = (
+    ("XT", 0, 0), ("XT", 0, 1), ("XE", 0, 0, "V"), ("XE", 0, 1, "S"), ("WR", 1), ("B3",),
+    ("B3C", "S"), ("XT", 1, 0), ("WQ", 1), ("XT", 1, 1), ("XE", 1, 0, "S"), ("XQ", 0),
+    ("XT", 2, 0), ("XE", 1, 1, "S"), ("BP", 0, 0), ("XE", 2, 0, "V"), ("BP", 0, 1), ("BE", 0, 0, "S"),
+    ("BP", 0, 2), ("WR", 0), ("BP", 0, 3), ("BE", 0, 1, "S"), ("XT", 2, 1), ("BE", 0, 2, "S"),
+    ("XQ", 1), ("BE", 0, 3, "S"), ("AT", 0, 0), ("WQ", 0), ("BP", 1, 0), ("XE", 2, 1, "S"),
+    ("BQ", 0), ("BP", 1, 1), ("BE", 1, 0, "S"), ("BP", 1, 2), ("XQ", 2), ("BP", 1, 3),
+    ("BE", 1, 1, "S"), ("AT", 0, 1), ("BE", 1, 2, "V"), ("AT", 0, 2), ("BE", 1, 3, "S"), ("BP", 2, 0),
+    ("AE", 0, 0, "S"), ("BQ", 1), ("BP", 2, 1), ("BP", 2, 2), ("AE", 0, 1, "S"), ("AQ", 0, 0),
+    ("BP", 2, 3), ("BE", 2, 0, "V"), ("AT", 1, 0), ("AE", 0, 2, "S"), ("AQ", 0, 1), ("AT", 1, 1),
+    ("BE", 2, 1, "S"), ("AQ", 0, 2), ("AT", 1, 2), ("BE", 2, 2, "V"), ("BE", 2, 3, "S"), ("DG", 0),
+    ("AE", 1, 0, "S"), ("BQ", 2), ("TP", 0), ("AE", 1, 1, "S"), ("AT", 2, 0), ("AQ", 1, 0),
+    ("S2", 0), ("AE", 1, 2, "S"), ("AQ", 1, 1), ("AE", 2, 0, "S"), ("AQ", 1, 2), ("AT", 2, 1),
+    ("U", 0), ("AT", 2, 2), ("AE", 2, 1, "S"), ("AQ", 2, 0), ("DG", 1), ("AE", 2, 2, "S"),
+    ("AQ", 2, 1), ("AT", 3, 0), ("AQ", 2, 2), ("AT", 3, 1), ("AE", 3, 0, "S"), ("AT", 3, 2),
+    ("DG", 2), ("AE", 3, 1, "S"), ("AQ", 3, 0), ("AE", 3, 2, "S"), ("AQ", 3, 1), ("TP", 1),
+    ("S2", 1), ("SLC", 0, "S"), ("AQ", 3, 2), ("SLM", 0), ("U", 1), ("TP", 2),
+    ("SLD", 0, "S"), ("S2", 2), ("Y", 0), ("Y", 1), ("AT", 4, 0), ("AT", 4, 1),
+    ("M", 0), ("AE", 4, 0, "S"), ("AT", 4, 2), ("M", 1), ("DG", 3), ("EX", 0),
+    ("U", 2), ("EX", 1), ("TP", 3), ("Y", 2), ("S2", 3), ("AE", 4, 1, "S"),
+    ("M", 2), ("AE", 4, 2, "S"), ("TP", 4), ("AQ", 4, 0), ("S2", 4), ("EX", 2),
+    ("AQ", 4, 1), ("AQ", 4, 2), ("U", 3), ("AT", 5, 0), ("AT", 5, 1), ("Y", 3),
+    ("AE", 5, 0, "S"), ("AT", 5, 2), ("M", 3), ("DG", 4), ("AE", 5, 1, "S"), ("U", 4),
+    ("EX", 3), ("TP", 5), ("Y", 4), ("S2", 5), ("AE", 5, 2, "S"), ("M", 4),
+    ("TP", 6), ("AQ", 5, 0), ("S2", 6), ("EX", 4), ("AQ", 5, 1), ("AQ", 5, 2),
+    ("DG", 5), ("U", 5), ("Y", 5), ("TP", 7), ("SLC", 1, "S"), ("M", 5),
+    ("S2", 7), ("U", 6), ("EX", 5), ("SLM", 1), ("U", 7), ("LN", 0, 6),
+    ("TP", 8), ("S2", 8), ("SLD", 1, "S"), ("SH", 0, 6), ("Y", 6), ("FN", 0, "G"),
+    ("TP", 9), ("Y", 7), ("FN", 1, "G"), ("M", 6), ("S2", 9), ("FN", 2, "G"),
+    ("M", 7), ("EX", 6), ("FN", 3, "G"), ("U", 8), ("TP", 10), ("Y", 8),
+    ("FN", 4, "G"), ("M", 8), ("S2", 10), ("FN", 5, "G"), ("U", 9), ("EX", 7),
+    ("TP", 11), ("Y", 9), ("EX", 8), ("M", 9), ("S2", 11), ("U", 10),
+    ("EX", 9), ("Y", 10), ("LN", 6, 10), ("M", 10), ("U", 11), ("Y", 11),
+    ("EX", 10), ("M", 11), ("SH", 6, 10), ("FN", 6, "G"), ("FN", 7, "G"), ("EX", 11),
+    ("FN", 8, "G"), ("LN", 10, 12), ("FN", 9, "G"), ("SH", 10, 12), ("FN", 10, "V"), ("FN", 11, "S"),
+)
 
 
 def tile_gcn_pc_kernel(tc, x_gc2, adj1, W3, b3, out):
     nc = tc.nc
     with ExitStack() as ctx:
         keep = ctx.enter_context(tc.tile_pool(name="keep", bufs=1))
-        grp_pool = ctx.enter_context(tc.tile_pool(name="grp", bufs=6))
-        work = ctx.enter_context(tc.tile_pool(name="work", bufs=3))
+        grp_pool = ctx.enter_context(tc.tile_pool(name="grp", bufs=9))
         junk = ctx.enter_context(tc.tile_pool(name="junk", bufs=2))
         ps_tr = ctx.enter_context(tc.psum_pool(name="pstr", bufs=3))
-        ps_acc = ctx.enter_context(tc.psum_pool(name="psacc", bufs=5))
+        ps_acc = ctx.enter_context(tc.psum_pool(name="psacc", bufs=4))
+        ps_deg = ctx.enter_context(tc.psum_pool(name="psdeg", bufs=1))
 
         x_v = x_gc2.rearrange("(a m e) k -> m a (e k)", a=NPAIR, m=P, e=2)
         adj_v = adj1.rearrange("(a m e) j -> m a (e j)", a=NPAIR, m=P, e=2)
@@ -55,8 +90,11 @@ def tile_gcn_pc_kernel(tc, x_gc2, adj1, W3, b3, out):
         adj_sb = [keep.tile([P, 2 * NODES], BF16, name="adj_sb%d" % a) for a in range(NPAIR)]
         adjq = [keep.tile([P, NG * 256], U32, name="adjq%d" % a, align_bytes=64) for a in range(NPAIR)]
         adjs = [keep.tile([P, NG * 256], U8, name="adjs%d" % a, align_bytes=64) for a in range(NPAIR)]
-        y_sb = [keep.tile([P, 2 * H], F32, name="y_sb%d" % a) for a in range(NPAIR)]
-        deg = [keep.tile([P, 1], F32, name="deg%d" % n) for n in range(NT)]
+        y_sb = [keep.tile([P, H], F32, name="y_sb%d" % n) for n in range(NT)]
+        part_sb = [keep.tile([P, 8 * RP], F32, name="part_sb%d" % r) for r in range(NPAIR // RP)]
+        deg_sb = [keep.tile([P, 2 * RP], F32, name="deg_sb%d" % r) for r in range(NPAIR // RP)]
+        fold = keep.tile([P, 32], F32, name="fold")
+        sel = keep.tile([P, 640], F32, name="sel")
         negm = keep.tile([P, NT], F32, name="negm")
         sums = keep.tile([P, NT], F32, name="sums")
         lns = keep.tile([P, NT], F32, name="lns")
@@ -67,199 +105,230 @@ def tile_gcn_pc_kernel(tc, x_gc2, adj1, W3, b3, out):
         b3bc = keep.tile([P, H], F32, name="b3bc")
         warm = keep.tile([P, 2], F32, name="warm")
 
-        nc.sync.dma_start(out=w_raw[1][:].rearrange("q (h f) -> q h f", h=2), in_=w_v[:, 1])
-        for g in range(NG):
-            nc.sync.dma_start(
-                out=x_sb[g][:].rearrange("m (a f) -> m a f", a=2), in_=x_v[:, 2 * g : 2 * g + 2, :]
-            )
-        nc.sync.dma_start(out=w_raw[0][:].rearrange("q (h f) -> q h f", h=2), in_=w_v[:, 0])
-        for a in range(NPAIR):
-            nc.sync.dma_start(out=adj_sb[a][:], in_=adj_v[:, a, :])
+        banks = {}
+        grouped = {}
 
-        nc.vector.memset(warm[:], 0.0)
-        nc.scalar.activation(out=warm[:, 1:2], in_=warm[:, 0:1], func=ACT.Exp)
-        make_identity(nc, ident[:])
-        nc.vector.memset(ones[:], 1.0)
-        nc.vector.memset(b3row[:], 0.0)
-        nc.scalar.dma_start(out=b3row[0:1, :], in_=b3.unsqueeze(0))
+        def copy_on(eng, dst, src):
+            if eng == "V":
+                nc.vector.tensor_copy(out=dst, in_=src)
+            else:
+                nc.scalar.copy(out=dst, in_=src)
 
-        def regroup_weights(w):
+        def op_wr(w):
             nc.vector.tensor_copy(
                 out=w_grp[w][:].rearrange("p (c i t) -> p c t i", c=P, i=4, t=4),
                 in_=w_raw[w][:].rearrange("p (t c i) -> p c t i", t=4, c=P, i=4),
             )
 
-        def quantise_weights(w):
+        def op_wq(w):
             nc.vector.quantize_mx(out=wq[w][:].bitcast(FP8X4), scales=ws[w][:], in_=w_grp[w][:])
 
-        def x_transposes(g):
+        def op_xt(g, b):
             words = x_sb[g][:].bitcast(F32)
-            grouped = x_grp[g][:].bitcast(F32)
-            for b in range(2):
-                bank = ps_tr.tile([P, H], F32, name="tr")
-                for n2 in range(2):
-                    for h in range(2):
-                        nc.tensor.transpose(
-                            bank[:, (2 * n2 + h) * P : (2 * n2 + h + 1) * P],
-                            words[:, (2 * b + n2) * 256 + h * P : (2 * b + n2) * 256 + (h + 1) * P],
-                            ident[:],
-                        )
-                nc.scalar.copy(
-                    out=grouped[:, b * H : (b + 1) * H].rearrange("q (n r h) -> q n r h", n=2, r=P, h=2),
-                    in_=bank[:].rearrange("q (n h r) -> q n r h", n=2, h=2, r=P),
-                )
+            bank = ps_tr.tile([P, H], F32, name="tr")
+            banks[("XT", g, b)] = bank
+            for n2 in range(2):
+                for h in range(2):
+                    col = (2 * b + n2) * 256 + h * P
+                    nc.tensor.transpose(bank[:, (2 * n2 + h) * P : (2 * n2 + h + 1) * P], words[:, col : col + P], ident[:])
 
-        def x_quantise(g):
+        def op_xe(g, b, eng):
+            copy_on(
+                eng,
+                x_grp[g][:].bitcast(F32)[:, b * H : (b + 1) * H].rearrange("q (n r h) -> q n r h", n=2, r=P, h=2),
+                banks[("XT", g, b)][:].rearrange("q (n h r) -> q n r h", n=2, h=2, r=P),
+            )
+
+        def op_xq(g):
             nc.vector.quantize_mx(out=xq[g][:].bitcast(FP8X4), scales=xs[g][:], in_=x_grp[g][:])
 
-        def bot_passes(g):
-            for cs in range(4):
-                bank = ps_acc.tile([P, H], F32, name="acc")
-                for t in range(4):
-                    nc.tensor.matmul_mx(
-                        out=bank[:, t * P : (t + 1) * P],
-                        lhsT=xq[g][:, t * P : (t + 1) * P].bitcast(FP8X4),
-                        lhsT_scale=xs[g][:, t * P : (t + 1) * P],
-                        rhs=wq[1][:, cs * P : (cs + 1) * P].bitcast(FP8X4),
-                        rhs_scale=ws[1][:, cs * P : (cs + 1) * P],
-                        start=True,
-                        stop=True,
-                    )
-                dst = bot_grp[g][:, cs * H : (cs + 1) * H].rearrange("m (c t) -> m c t", c=P, t=4)
-                src = bank[:].rearrange("m (t c) -> m c t", t=4, c=P)
-                if cs in BOT_EVAC_ON_VECTOR:
-                    nc.vector.tensor_copy(out=dst, in_=src)
-                else:
-                    nc.scalar.copy(out=dst, in_=src)
-
-        def bot_quantise(g):
-            nc.vector.quantize_mx(out=botq[g][:].bitcast(FP8X4), scales=bots[g][:], in_=bot_grp[g][:])
-
-        def adj_stage(a):
-            words = adj_sb[a][:].bitcast(F32)
-            grouped = []
-            for g in range(NG):
-                bank = ps_tr.tile([P, H], F32, name="tr")
-                for e in range(2):
-                    for u in range(2):
-                        col = e * 768 + g * 256 + u * P
-                        nc.tensor.transpose(
-                            bank[:, (2 * e + u) * P : (2 * e + u + 1) * P], words[:, col : col + P], ident[:]
-                        )
-                agrp = grp_pool.tile([P, 2 * H], BF16, name="agrp", align_bytes=64)
-                nc.scalar.copy(
-                    out=agrp[:].bitcast(F32).rearrange("q (e i u) -> q e i u", e=2, i=P, u=2),
-                    in_=bank[:].rearrange("q (e u i) -> q e i u", e=2, u=2, i=P),
-                )
-                grouped.append(agrp)
-            for e in range(2):
-                n = 2 * a + e
-                rows = adj_sb[a][:, e * NODES : (e + 1) * NODES]
-                dj = junk.tile([P, NODES], BF16, name="dj")
-                if n in DEG_ON_VECTOR:
-                    nc.vector.tensor_scalar(
-                        out=dj[:], in0=rows, scalar1=1.0, scalar2=None, op0=ALU.mult, op1=ALU.add,
-                        accum_out=deg[n][:],
-                    )
-                else:
-                    nc.scalar.activation(out=dj[:], in_=rows, func=ACT.Copy, accum_out=deg[n][:])
-            for g in range(NG):
-                nc.vector.quantize_mx(
-                    out=adjq[a][:, g * 256 : (g + 1) * 256].bitcast(FP8X4),
-                    scales=adjs[a][:, g * 256 : (g + 1) * 256],
-                    in_=grouped[g][:],
-                )
-
-        def epilogue(a):
-            tops = []
-            abs_ = []
-            for e in range(2):
-                n = 2 * a + e
-                g0, t0 = n // 4, n % 4
-                top_ps = ps_acc.tile([P, H], F32, name="acc")
+        def op_bp(g, cs):
+            bank = ps_acc.tile([P, H], F32, name="acc")
+            banks[("BP", g, cs)] = bank
+            for t in range(4):
                 nc.tensor.matmul_mx(
-                    out=top_ps[:],
-                    lhsT=xq[g0][:, t0 * P : (t0 + 1) * P].bitcast(FP8X4),
-                    lhsT_scale=xs[g0][:, t0 * P : (t0 + 1) * P],
-                    rhs=wq[0][:].bitcast(FP8X4),
-                    rhs_scale=ws[0][:],
+                    out=bank[:, t * P : (t + 1) * P],
+                    lhsT=xq[g][:, t * P : (t + 1) * P].bitcast(FP8X4),
+                    lhsT_scale=xs[g][:, t * P : (t + 1) * P],
+                    rhs=wq[1][:, cs * P : (cs + 1) * P].bitcast(FP8X4),
+                    rhs_scale=ws[1][:, cs * P : (cs + 1) * P],
                     start=True,
                     stop=True,
                 )
-                ab_ps = ps_acc.tile([P, H], F32, name="acc")
-                for g in range(NG):
-                    col = g * 256 + e * P
-                    nc.tensor.matmul_mx(
-                        out=ab_ps[:],
-                        lhsT=adjq[a][:, col : col + P].bitcast(FP8X4),
-                        lhsT_scale=adjs[a][:, col : col + P],
-                        rhs=botq[g][:].bitcast(FP8X4),
-                        rhs_scale=bots[g][:],
-                        start=(g == 0),
-                        stop=(g == NG - 1),
-                    )
-                tops.append(top_ps)
-                abs_.append(ab_ps)
+
+        def op_be(g, cs, eng):
+            copy_on(
+                eng,
+                bot_grp[g][:, cs * H : (cs + 1) * H].rearrange("m (c t) -> m c t", c=P, t=4),
+                banks[("BP", g, cs)][:].rearrange("m (t c) -> m c t", t=4, c=P),
+            )
+
+        def op_bq(g):
+            nc.vector.quantize_mx(out=botq[g][:].bitcast(FP8X4), scales=bots[g][:], in_=bot_grp[g][:])
+
+        def op_b3():
+            bank = ps_tr.tile([P, H], F32, name="tr")
+            banks[("B3",)] = bank
+            nc.tensor.matmul(out=bank[:], lhsT=ones[:], rhs=b3row[:], start=True, stop=True)
+
+        def op_b3c(eng):
+            copy_on(eng, b3bc[:], banks[("B3",)][:])
+
+        def op_at(a, g):
+            words = adj_sb[a][:].bitcast(F32)
+            bank = ps_tr.tile([P, H], F32, name="tr")
+            banks[("AT", a, g)] = bank
             for e in range(2):
-                n = 2 * a + e
-                y = y_sb[a][:, e * H : (e + 1) * H]
-                t1 = work.tile([P, H], F32, name="t1")
-                nc.vector.scalar_tensor_tensor(
-                    out=t1[:], in0=tops[e][:], scalar=deg[n][:], in1=b3bc[:], op0=ALU.mult, op1=ALU.add
-                )
-                nc.vector.tensor_tensor(out=y, in0=abs_[e][:], in1=t1[:], op=ALU.add)
-                nc.vector.tensor_reduce(out=negm[:, n : n + 1], in_=y, axis=AX.X, op=ALU.max, negate=True)
-                ej = junk.tile([P, H], BF16, name="ej")
-                nc.scalar.activation(
-                    out=ej[:], in_=y, func=ACT.Exp, bias=negm[:, n : n + 1], scale=1.0,
-                    accum_out=sums[:, n : n + 1],
+                for u in range(2):
+                    col = e * 768 + g * 256 + u * P
+                    nc.tensor.transpose(bank[:, (2 * e + u) * P : (2 * e + u + 1) * P], words[:, col : col + P], ident[:])
+
+        def op_ae(a, g, eng):
+            agrp = grp_pool.tile([P, 2 * H], BF16, name="agrp", align_bytes=64)
+            grouped[(a, g)] = agrp
+            copy_on(
+                eng,
+                agrp[:].bitcast(F32).rearrange("q (e i u) -> q e i u", e=2, i=P, u=2),
+                banks[("AT", a, g)][:].rearrange("q (e u i) -> q e i u", e=2, u=2, i=P),
+            )
+
+        def op_aq(a, g):
+            nc.vector.quantize_mx(
+                out=adjq[a][:, g * 256 : (g + 1) * 256].bitcast(FP8X4),
+                scales=adjs[a][:, g * 256 : (g + 1) * 256],
+                in_=grouped[(a, g)][:],
+            )
+
+        def op_dg(a):
+            r = a // RP
+            if a % RP == 0:
+                banks[("PART", r)] = ps_deg.tile([P, H], F32, name="part")
+            part = banks[("PART", r)]
+            for e in range(2):
+                nl = 2 * (a % RP) + e
+                for s in range(4):
+                    col = 2 * RP * s + nl
+                    for g in range(NG):
+                        nc.tensor.matmul(
+                            out=part[:, col : col + 1],
+                            lhsT=grouped[(a, g)][:, e * H + s * P : e * H + (s + 1) * P],
+                            rhs=ones[:, 0:1],
+                            start=(g == 0),
+                            stop=(g == NG - 1),
+                        )
+
+        def op_slc(r, eng):
+            copy_on(eng, part_sb[r][:], banks[("PART", r)][:, 0 : 8 * RP])
+
+        def op_slm(r):
+            for s in range(4):
+                nc.tensor.matmul(
+                    out=banks[("PART", r)][:, 256 : 256 + 2 * RP],
+                    lhsT=sel[:, s * P : (s + 1) * P],
+                    rhs=part_sb[r][:, 2 * RP * s : 2 * RP * (s + 1)],
+                    start=(s == 0),
+                    stop=(s == 3),
                 )
 
-        def finish(lo, hi, last):
+        def op_sld(r, eng):
+            copy_on(eng, deg_sb[r][:], banks[("PART", r)][:, 256 : 256 + 2 * RP])
+
+        def op_s2(n):
+            a, e = n // 2, n % 2
+            bank = ps_acc.tile([P, H], F32, name="acc")
+            banks[("S2", n)] = bank
+            for g in range(NG):
+                col = g * 256 + e * P
+                nc.tensor.matmul_mx(
+                    out=bank[:],
+                    lhsT=adjq[a][:, col : col + P].bitcast(FP8X4),
+                    lhsT_scale=adjs[a][:, col : col + P],
+                    rhs=botq[g][:].bitcast(FP8X4),
+                    rhs_scale=bots[g][:],
+                    start=(g == 0),
+                    stop=(g == NG - 1),
+                )
+
+        def op_u(n):
+            nc.vector.tensor_tensor(out=y_sb[n][:], in0=banks[("S2", n)][:], in1=b3bc[:], op=ALU.add)
+
+        def op_tp(n):
+            g0, t0 = n // 4, n % 4
+            bank = ps_acc.tile([P, H], F32, name="acc")
+            banks[("TP", n)] = bank
+            nc.tensor.matmul_mx(
+                out=bank[:],
+                lhsT=xq[g0][:, t0 * P : (t0 + 1) * P].bitcast(FP8X4),
+                lhsT_scale=xs[g0][:, t0 * P : (t0 + 1) * P],
+                rhs=wq[0][:].bitcast(FP8X4),
+                rhs_scale=ws[0][:],
+                start=True,
+                stop=True,
+            )
+
+        def op_y(n):
+            r, nl = n // (2 * RP), n % (2 * RP)
+            nc.vector.scalar_tensor_tensor(
+                out=y_sb[n][:], in0=banks[("TP", n)][:], scalar=deg_sb[r][:, nl : nl + 1], in1=y_sb[n][:],
+                op0=ALU.mult, op1=ALU.add,
+            )
+
+        def op_m(n):
+            nc.vector.tensor_reduce(out=negm[:, n : n + 1], in_=y_sb[n][:], axis=AX.X, op=ALU.max, negate=True)
+
+        def op_ex(n):
+            ej = junk.tile([P, H], BF16, name="ej")
+            nc.scalar.activation(
+                out=ej[:], in_=y_sb[n][:], func=ACT.Exp, bias=negm[:, n : n + 1], scale=1.0,
+                accum_out=sums[:, n : n + 1],
+            )
+
+        def op_ln(lo, hi):
             nc.scalar.activation(out=lns[:, lo:hi], in_=sums[:, lo:hi], func=ACT.Ln)
-            nc.vector.tensor_tensor(out=shift[:, lo:hi], in0=negm[:, lo:hi], in1=lns[:, lo:hi], op=ALU.subtract)
-            for n in range(lo, hi):
-                a, e = n // 2, n % 2
-                y = y_sb[a][:, e * H : (e + 1) * H]
-                if last and e == 0:
-                    nc.vector.tensor_scalar(
-                        out=y, in0=y, scalar1=shift[:, n : n + 1], scalar2=None, op0=ALU.add
-                    )
-                elif last:
-                    nc.scalar.activation(out=y, in_=y, func=ACT.Identity, bias=shift[:, n : n + 1], scale=1.0)
-                else:
-                    nc.gpsimd.tensor_scalar(
-                        out=y, in0=y, scalar1=1.0, scalar2=shift[:, n : n + 1], op0=ALU.mult, op1=ALU.add
-                    )
-                nc.sync.dma_start(out=out_v[:, a, e * H : (e + 1) * H], in_=y)
 
-        regroup_weights(1)
-        x_transposes(0)
-        quantise_weights(1)
-        x_transposes(1)
-        x_quantise(0)
-        bot_passes(0)
-        x_transposes(2)
-        x_quantise(1)
-        bot_passes(1)
-        x_quantise(2)
-        bot_quantise(0)
-        bot_passes(2)
-        b3_ps = ps_tr.tile([P, H], F32, name="tr")
-        nc.tensor.matmul(out=b3_ps[:], lhsT=ones[:], rhs=b3row[:], start=True, stop=True)
-        nc.scalar.copy(out=b3bc[:], in_=b3_ps[:])
-        regroup_weights(0)
-        bot_quantise(1)
-        adj_stage(0)
-        bot_quantise(2)
-        quantise_weights(0)
-        adj_stage(1)
-        grp = 0
-        for a in range(NPAIR):
-            if a + 2 < NPAIR:
-                adj_stage(a + 2)
-            epilogue(a)
-            lo, hi = LN_GROUPS[grp]
-            if 2 * a + 2 == hi:
-                finish(lo, hi, grp == len(LN_GROUPS) - 1)
-                grp += 1
+        def op_sh(lo, hi):
+            nc.vector.tensor_tensor(out=shift[:, lo:hi], in0=negm[:, lo:hi], in1=lns[:, lo:hi], op=ALU.subtract)
+
+        def op_fn(n, eng):
+            y = y_sb[n][:]
+            if eng == "V":
+                nc.vector.tensor_scalar(out=y, in0=y, scalar1=shift[:, n : n + 1], scalar2=None, op0=ALU.add)
+            elif eng == "S":
+                nc.scalar.activation(out=y, in_=y, func=ACT.Identity, bias=shift[:, n : n + 1], scale=1.0)
+            else:
+                nc.gpsimd.tensor_scalar(out=y, in0=y, scalar1=1.0, scalar2=shift[:, n : n + 1], op0=ALU.mult, op1=ALU.add)
+            nc.sync.dma_start(out=out_v[:, n // 2, (n % 2) * H : (n % 2 + 1) * H], in_=y)
+
+        ops = {
+            "WR": op_wr, "WQ": op_wq, "XT": op_xt, "XE": op_xe, "XQ": op_xq, "BP": op_bp, "BE": op_be, "BQ": op_bq,
+            "B3": op_b3, "B3C": op_b3c, "AT": op_at, "AE": op_ae, "AQ": op_aq, "DG": op_dg, "SLC": op_slc,
+            "SLM": op_slm, "SLD": op_sld, "S2": op_s2, "U": op_u, "TP": op_tp, "Y": op_y, "M": op_m, "EX": op_ex,
+            "LN": op_ln, "SH": op_sh, "FN": op_fn,
+        }
+
+        with tc.manual_schedule():
+            nc.vector.memset(b3row[:], 0.0)
+            nc.scalar.dma_start(out=b3row[0:1, :], in_=b3.unsqueeze(0))
+            for kind, i in LOADS:
+                if kind == "x":
+                    nc.sync.dma_start(
+                        out=x_sb[i][:].rearrange("m (a f) -> m a f", a=2), in_=x_v[:, 2 * i : 2 * i + 2, :]
+                    )
+                elif kind == "w":
+                    nc.sync.dma_start(out=w_raw[i][:].rearrange("q (h f) -> q h f", h=2), in_=w_v[:, i])
+                else:
+                    nc.sync.dma_start(out=adj_sb[i][:], in_=adj_v[:, i, :])
+            nc.vector.memset(warm[:], 0.0)
+            nc.scalar.activation(out=warm[:, 1:2], in_=warm[:, 0:1], func=ACT.Exp)
+            make_identity(nc, ident[:])
+            nc.vector.memset(ones[:], 1.0)
+            nc.vector.memset(sel[:], 0.0)
+            nc.vector.tensor_reduce(
+                out=fold[:], in_=ident[:].rearrange("q (r t) -> q r t", r=32, t=4), axis=AX.X, op=ALU.add
+            )
+            nc.vector.tensor_copy(
+                out=sel[:].rearrange("q (s w) -> q s w", s=4, w=160)[:, :, 0:32],
+                in_=fold[:].unsqueeze(1).to_broadcast([P, 4, 32]),
+            )
+            for step in ORDER:
+                ops[step[0]](*step[1:])

@@ -24,40 +24,40 @@ RP = 3
 LOADS = (("x", 0), ("w", 1), ("x", 1), ("x", 2), ("w", 0), ("a", 0), ("a", 1), ("a", 2), ("a", 3), ("a", 4), ("a", 5))
 
 ORDER = (
-    ("XT", 0, 0), ("XT", 0, 1), ("XE", 0, 0, "V"), ("XE", 0, 1, "S"), ("WR", 1), ("B3",),
-    ("B3C", "S"), ("XT", 1, 0), ("WQ", 1), ("XT", 1, 1), ("XE", 1, 0, "S"), ("XQ", 0),
-    ("XT", 2, 0), ("XE", 1, 1, "S"), ("BP", 0, 0), ("XE", 2, 0, "V"), ("BP", 0, 1), ("BE", 0, 0, "S"),
-    ("BP", 0, 2), ("WR", 0), ("BP", 0, 3), ("BE", 0, 1, "S"), ("XT", 2, 1), ("BE", 0, 2, "S"),
-    ("XQ", 1), ("BE", 0, 3, "S"), ("AT", 0, 0), ("WQ", 0), ("BP", 1, 0), ("XE", 2, 1, "S"),
-    ("BQ", 0), ("BP", 1, 1), ("BE", 1, 0, "S"), ("BP", 1, 2), ("XQ", 2), ("BP", 1, 3),
-    ("BE", 1, 1, "S"), ("AT", 0, 1), ("BE", 1, 2, "V"), ("AT", 0, 2), ("BE", 1, 3, "S"), ("BP", 2, 0),
-    ("AE", 0, 0, "S"), ("BQ", 1), ("BP", 2, 1), ("BP", 2, 2), ("AE", 0, 1, "S"), ("AQ", 0, 0),
-    ("BP", 2, 3), ("BE", 2, 0, "V"), ("AT", 1, 0), ("AE", 0, 2, "S"), ("AQ", 0, 1), ("AT", 1, 1),
-    ("BE", 2, 1, "S"), ("AQ", 0, 2), ("AT", 1, 2), ("BE", 2, 2, "V"), ("BE", 2, 3, "S"), ("DG", 0),
-    ("AE", 1, 0, "S"), ("BQ", 2), ("TP", 0), ("AE", 1, 1, "S"), ("AT", 2, 0), ("AQ", 1, 0),
-    ("S2", 0), ("AE", 1, 2, "S"), ("AQ", 1, 1), ("AE", 2, 0, "S"), ("AQ", 1, 2), ("AT", 2, 1),
-    ("U", 0), ("AT", 2, 2), ("AE", 2, 1, "S"), ("AQ", 2, 0), ("DG", 1), ("AE", 2, 2, "S"),
-    ("AQ", 2, 1), ("AT", 3, 0), ("AQ", 2, 2), ("AT", 3, 1), ("AE", 3, 0, "S"), ("AT", 3, 2),
-    ("DG", 2), ("AE", 3, 1, "S"), ("AQ", 3, 0), ("AE", 3, 2, "S"), ("AQ", 3, 1), ("TP", 1),
-    ("S2", 1), ("SLC", 0, "S"), ("AQ", 3, 2), ("SLM", 0), ("U", 1), ("TP", 2),
-    ("SLD", 0, "S"), ("S2", 2), ("Y", 0), ("Y", 1), ("AT", 4, 0), ("AT", 4, 1),
-    ("M", 0), ("AE", 4, 0, "S"), ("AT", 4, 2), ("M", 1), ("DG", 3), ("EX", 0),
-    ("U", 2), ("EX", 1), ("TP", 3), ("Y", 2), ("S2", 3), ("AE", 4, 1, "S"),
-    ("M", 2), ("AE", 4, 2, "S"), ("TP", 4), ("AQ", 4, 0), ("S2", 4), ("EX", 2),
-    ("AQ", 4, 1), ("AQ", 4, 2), ("U", 3), ("AT", 5, 0), ("AT", 5, 1), ("Y", 3),
-    ("AE", 5, 0, "S"), ("AT", 5, 2), ("M", 3), ("DG", 4), ("AE", 5, 1, "S"), ("U", 4),
-    ("EX", 3), ("TP", 5), ("Y", 4), ("S2", 5), ("AE", 5, 2, "S"), ("M", 4),
-    ("TP", 6), ("AQ", 5, 0), ("S2", 6), ("EX", 4), ("AQ", 5, 1), ("AQ", 5, 2),
-    ("DG", 5), ("U", 5), ("Y", 5), ("TP", 7), ("SLC", 1, "S"), ("M", 5),
-    ("S2", 7), ("U", 6), ("EX", 5), ("SLM", 1), ("U", 7), ("LN", 0, 6),
-    ("TP", 8), ("S2", 8), ("SLD", 1, "S"), ("SH", 0, 6), ("Y", 6), ("FN", 0, "G"),
-    ("TP", 9), ("Y", 7), ("FN", 1, "G"), ("M", 6), ("S2", 9), ("FN", 2, "G"),
-    ("M", 7), ("EX", 6), ("FN", 3, "G"), ("U", 8), ("TP", 10), ("Y", 8),
-    ("FN", 4, "G"), ("M", 8), ("S2", 10), ("FN", 5, "G"), ("U", 9), ("EX", 7),
-    ("TP", 11), ("Y", 9), ("EX", 8), ("M", 9), ("S2", 11), ("U", 10),
-    ("EX", 9), ("Y", 10), ("LN", 6, 10), ("M", 10), ("U", 11), ("Y", 11),
-    ("EX", 10), ("M", 11), ("SH", 6, 10), ("FN", 6, "G"), ("FN", 7, "G"), ("EX", 11),
-    ("FN", 8, "G"), ("LN", 10, 12), ("FN", 9, "G"), ("SH", 10, 12), ("FN", 10, "V"), ("FN", 11, "S"),
+    ("XT", 0, 0), ("XT", 0, 1), ("XE", 0, 0, "S"), ("WR", 1), ("XE", 0, 1, "S"), ("B3",),
+    ("B3C", "S"), ("XT", 1, 1), ("XQ", 0), ("XT", 1, 0), ("XE", 1, 1, "S"), ("WQ", 1),
+    ("XT", 2, 0), ("XE", 1, 0, "S"), ("BP", 0, 0), ("XQ", 1), ("BP", 0, 1), ("BE", 0, 0, "S"),
+    ("BP", 0, 2), ("XE", 2, 0, "V"), ("XT", 2, 1), ("BE", 0, 1, "S"), ("BE", 0, 2, "V"), ("BP", 1, 0),
+    ("XE", 2, 1, "S"), ("BP", 0, 3), ("WR", 0), ("BP", 1, 3), ("BE", 1, 0, "S"), ("BP", 1, 1),
+    ("AT", 0, 1), ("BE", 0, 3, "S"), ("XQ", 2), ("AT", 0, 0), ("BE", 1, 3, "S"), ("AT", 0, 2),
+    ("BE", 1, 1, "V"), ("BP", 1, 2), ("AE", 0, 1, "S"), ("BQ", 0), ("BP", 2, 0), ("BE", 1, 2, "S"),
+    ("BP", 2, 1), ("WQ", 0), ("BP", 2, 2), ("AE", 0, 0, "S"), ("BP", 2, 3), ("BE", 2, 1, "V"),
+    ("AT", 1, 0), ("AE", 0, 2, "S"), ("AT", 1, 1), ("BE", 2, 0, "S"), ("AE", 1, 0, "V"), ("AT", 1, 2),
+    ("DG", 0), ("AQ", 0, 2), ("AE", 1, 2, "S"), ("AQ", 0, 1), ("AQ", 0, 0), ("AE", 1, 1, "S"),
+    ("TP", 0), ("BE", 2, 3, "V"), ("AT", 2, 2), ("BE", 2, 2, "S"), ("BQ", 1), ("AT", 2, 0),
+    ("AT", 2, 1), ("AQ", 1, 2), ("AE", 2, 0, "S"), ("DG", 1), ("BQ", 2), ("AE", 2, 2, "S"),
+    ("TP", 1), ("AE", 2, 1, "S"), ("S2", 0), ("DG", 2), ("U", 0), ("AQ", 2, 1),
+    ("S2", 1), ("AQ", 2, 2), ("SLC", 0, "S"), ("AQ", 1, 0), ("SLM", 0), ("U", 1),
+    ("AQ", 2, 0), ("AQ", 1, 1), ("AT", 3, 0), ("SLD", 0, "S"), ("AT", 3, 2), ("Y", 0),
+    ("AE", 3, 0, "S"), ("AT", 3, 1), ("Y", 1), ("AE", 3, 2, "S"), ("AT", 4, 1), ("S2", 2),
+    ("AQ", 3, 0), ("AE", 3, 1, "S"), ("M", 1), ("AQ", 3, 2), ("TP", 2), ("U", 2),
+    ("S2", 3), ("M", 0), ("TP", 3), ("TP", 4), ("Y", 2), ("EX", 0),
+    ("AT", 4, 2), ("U", 3), ("AT", 4, 0), ("AE", 4, 2, "S"), ("S2", 4), ("M", 2),
+    ("AE", 4, 0, "S"), ("Y", 3), ("S2", 5), ("AE", 4, 1, "S"), ("U", 4), ("EX", 1),
+    ("TP", 5), ("AQ", 3, 1), ("DG", 3), ("AQ", 4, 1), ("EX", 2), ("M", 3),
+    ("AT", 5, 0), ("U", 5), ("AT", 5, 1), ("AE", 5, 0, "S"), ("Y", 4), ("DG", 4),
+    ("AE", 5, 1, "S"), ("AQ", 4, 0), ("Y", 5), ("AT", 5, 2), ("EX", 3), ("S2", 6),
+    ("M", 4), ("AE", 5, 2, "S"), ("M", 5), ("EX", 4), ("TP", 7), ("DG", 5),
+    ("AQ", 5, 0), ("EX", 5), ("S2", 7), ("SLC", 1, "V"), ("LN", 0, 6), ("U", 6),
+    ("SLM", 1), ("AQ", 5, 1), ("U", 7), ("AQ", 5, 2), ("TP", 6), ("AQ", 4, 2),
+    ("SLD", 1, "S"), ("SH", 0, 6), ("S2", 8), ("Y", 6), ("FN", 0, "G"), ("Y", 7),
+    ("FN", 1, "G"), ("M", 6), ("S2", 9), ("FN", 2, "G"), ("M", 7), ("TP", 9),
+    ("U", 8), ("FN", 3, "G"), ("TP", 8), ("EX", 7), ("U", 9), ("S2", 10),
+    ("FN", 4, "G"), ("Y", 8), ("TP", 11), ("FN", 5, "G"), ("Y", 9), ("M", 8),
+    ("EX", 6), ("S2", 11), ("M", 9), ("EX", 8), ("TP", 10), ("U", 10),
+    ("EX", 9), ("Y", 10), ("LN", 6, 10), ("M", 10), ("U", 11), ("EX", 10),
+    ("SH", 6, 10), ("Y", 11), ("FN", 6, "G"), ("FN", 7, "G"), ("M", 11), ("FN", 8, "G"),
+    ("EX", 11), ("FN", 9, "G"), ("LN", 10, 12), ("SH", 10, 12), ("FN", 10, "G"), ("FN", 11, "V"),
 )
 
 

@@ -20,44 +20,44 @@ NODES = 1536
 NG = 3
 NPAIR = 6
 NT = 12
-RP = 3
 LOADS = (("x", 0), ("w", 1), ("x", 1), ("x", 2), ("w", 0), ("a", 0), ("a", 1), ("a", 2), ("a", 3), ("a", 4), ("a", 5))
 
 ORDER = (
-    ("XT", 0, 0), ("XT", 0, 1), ("XE", 0, 0, "S"), ("WR", 1), ("XE", 0, 1, "S"), ("B3",),
-    ("B3C", "S"), ("XT", 1, 1), ("XQ", 0), ("XT", 1, 0), ("XE", 1, 1, "S"), ("WQ", 1),
-    ("XT", 2, 0), ("XE", 1, 0, "S"), ("BP", 0, 0), ("XQ", 1), ("BP", 0, 1), ("BE", 0, 0, "S"),
-    ("BP", 0, 2), ("XE", 2, 0, "V"), ("XT", 2, 1), ("BE", 0, 1, "S"), ("BE", 0, 2, "V"), ("BP", 1, 0),
-    ("XE", 2, 1, "S"), ("BP", 0, 3), ("WR", 0), ("BP", 1, 3), ("BE", 1, 0, "S"), ("BP", 1, 1),
-    ("AT", 0, 1), ("BE", 0, 3, "S"), ("XQ", 2), ("AT", 0, 0), ("BE", 1, 3, "S"), ("AT", 0, 2),
-    ("BE", 1, 1, "V"), ("BP", 1, 2), ("AE", 0, 1, "S"), ("BQ", 0), ("BP", 2, 0), ("BE", 1, 2, "S"),
-    ("BP", 2, 1), ("WQ", 0), ("BP", 2, 2), ("AE", 0, 0, "S"), ("BP", 2, 3), ("BE", 2, 1, "V"),
-    ("AT", 1, 0), ("AE", 0, 2, "S"), ("AT", 1, 1), ("BE", 2, 0, "S"), ("AE", 1, 0, "V"), ("AT", 1, 2),
-    ("DG", 0), ("AQ", 0, 2), ("AE", 1, 2, "S"), ("AQ", 0, 1), ("AQ", 0, 0), ("AE", 1, 1, "S"),
-    ("TP", 0), ("BE", 2, 3, "V"), ("AT", 2, 2), ("BE", 2, 2, "S"), ("BQ", 1), ("AT", 2, 0),
-    ("AT", 2, 1), ("AQ", 1, 2), ("AE", 2, 0, "S"), ("DG", 1), ("BQ", 2), ("AE", 2, 2, "S"),
-    ("TP", 1), ("AE", 2, 1, "S"), ("S2", 0), ("DG", 2), ("U", 0), ("AQ", 2, 1),
-    ("S2", 1), ("AQ", 2, 2), ("SLC", 0, "S"), ("AQ", 1, 0), ("SLM", 0), ("U", 1),
-    ("AQ", 2, 0), ("AQ", 1, 1), ("AT", 3, 0), ("SLD", 0, "S"), ("AT", 3, 2), ("Y", 0),
-    ("AE", 3, 0, "S"), ("AT", 3, 1), ("Y", 1), ("AE", 3, 2, "S"), ("AT", 4, 1), ("S2", 2),
-    ("AQ", 3, 0), ("AE", 3, 1, "S"), ("M", 1), ("AQ", 3, 2), ("TP", 2), ("U", 2),
-    ("S2", 3), ("M", 0), ("TP", 3), ("TP", 4), ("Y", 2), ("EX", 0),
-    ("AT", 4, 2), ("U", 3), ("AT", 4, 0), ("AE", 4, 2, "S"), ("S2", 4), ("M", 2),
-    ("AE", 4, 0, "S"), ("Y", 3), ("S2", 5), ("AE", 4, 1, "S"), ("U", 4), ("EX", 1),
-    ("TP", 5), ("AQ", 3, 1), ("DG", 3), ("AQ", 4, 1), ("EX", 2), ("M", 3),
-    ("AT", 5, 0), ("U", 5), ("AT", 5, 1), ("AE", 5, 0, "S"), ("Y", 4), ("DG", 4),
-    ("AE", 5, 1, "S"), ("AQ", 4, 0), ("Y", 5), ("AT", 5, 2), ("EX", 3), ("S2", 6),
-    ("M", 4), ("AE", 5, 2, "S"), ("M", 5), ("EX", 4), ("TP", 7), ("DG", 5),
-    ("AQ", 5, 0), ("EX", 5), ("S2", 7), ("SLC", 1, "V"), ("LN", 0, 6), ("U", 6),
-    ("SLM", 1), ("AQ", 5, 1), ("U", 7), ("AQ", 5, 2), ("TP", 6), ("AQ", 4, 2),
-    ("SLD", 1, "S"), ("SH", 0, 6), ("S2", 8), ("Y", 6), ("FN", 0, "G"), ("Y", 7),
-    ("FN", 1, "G"), ("M", 6), ("S2", 9), ("FN", 2, "G"), ("M", 7), ("TP", 9),
-    ("U", 8), ("FN", 3, "G"), ("TP", 8), ("EX", 7), ("U", 9), ("S2", 10),
-    ("FN", 4, "G"), ("Y", 8), ("TP", 11), ("FN", 5, "G"), ("Y", 9), ("M", 8),
-    ("EX", 6), ("S2", 11), ("M", 9), ("EX", 8), ("TP", 10), ("U", 10),
-    ("EX", 9), ("Y", 10), ("LN", 6, 10), ("M", 10), ("U", 11), ("EX", 10),
-    ("SH", 6, 10), ("Y", 11), ("FN", 6, "G"), ("FN", 7, "G"), ("M", 11), ("FN", 8, "G"),
-    ("EX", 11), ("FN", 9, "G"), ("LN", 10, 12), ("SH", 10, 12), ("FN", 10, "G"), ("FN", 11, "V"),
+    ("XT", 0, 0), ("XT", 0, 1), ("XE", 0, 1, "S"), ("WR", 1), ("B3",), ("XE", 0, 0, "S"),
+    ("B3C", "S"), ("XT", 1, 1), ("XQ", 0), ("XT", 1, 0), ("WQ", 1), ("XE", 1, 0, "S"),
+    ("XT", 2, 0), ("BP", 0, 0), ("XE", 1, 1, "S"), ("XE", 2, 0, "V"), ("BP", 0, 3), ("BE", 0, 0, "S"),
+    ("BP", 0, 2), ("WR", 0), ("BP", 0, 1), ("BE", 0, 3, "S"), ("XT", 2, 1), ("BE", 0, 2, "S"),
+    ("XQ", 1), ("BE", 0, 1, "S"), ("AT", 0, 2), ("DV", 0, "V"), ("BP", 1, 0), ("XE", 2, 1, "S"),
+    ("BP", 1, 1), ("WQ", 0), ("BP", 1, 2), ("BE", 1, 1, "S"), ("BP", 1, 3), ("BQ", 0),
+    ("TP", 0), ("BE", 1, 0, "S"), ("AT", 0, 0), ("XQ", 2), ("BE", 1, 3, "S"), ("AT", 0, 1),
+    ("DV", 2, "V"), ("AT", 1, 2), ("BE", 1, 2, "S"), ("DF", 1), ("AE", 0, 0, "S"), ("DV", 4, "V"),
+    ("BP", 2, 1), ("AE", 0, 2, "S"), ("BP", 2, 0), ("BQ", 1), ("BP", 2, 2), ("AE", 0, 1, "S"),
+    ("TP", 1), ("DR", 1, "V"), ("BE", 2, 0, "S"), ("BP", 2, 3), ("U", 0), ("AT", 1, 1),
+    ("BE", 2, 2, "S"), ("AQ", 0, 0), ("DF", 3), ("AQ", 0, 1), ("BE", 2, 3, "S"), ("DV", 6, "V"),
+    ("BE", 2, 1, "S"), ("TP", 2), ("AT", 1, 0), ("U", 1), ("AE", 1, 1, "S"), ("DF", 5),
+    ("BQ", 2), ("DR", 3, "S"), ("AE", 1, 2, "S"), ("TP", 7), ("AQ", 0, 2), ("TP", 3),
+    ("AE", 1, 0, "S"), ("U", 2), ("S2", 0), ("DV", 8, "S"), ("DR", 5, "V"), ("AQ", 1, 2),
+    ("TP", 4), ("AQ", 1, 1), ("S2", 1), ("AQ", 1, 0), ("U", 3), ("S2", 2),
+    ("Y", 0), ("U", 4), ("S2", 3), ("Y", 1), ("TP", 6), ("Y", 2),
+    ("AT", 2, 2), ("AT", 2, 0), ("Y", 3), ("AT", 3, 2), ("AE", 2, 0, "S"), ("M", 0),
+    ("AT", 2, 1), ("DF", 7), ("U", 6), ("AE", 2, 1, "S"), ("M", 1), ("AE", 2, 2, "S"),
+    ("TP", 5), ("TP", 8), ("AQ", 2, 1), ("AE", 3, 2, "S"), ("DF", 9), ("M", 3),
+    ("DR", 7, "S"), ("EX", 0), ("U", 8), ("AT", 3, 0), ("AT", 4, 0), ("AQ", 2, 0),
+    ("AE", 3, 0, "S"), ("AT", 4, 1), ("AQ", 2, 2), ("AT", 3, 1), ("U", 5), ("AE", 4, 0, "S"),
+    ("S2", 4), ("EX", 3), ("U", 7), ("AQ", 3, 0), ("EX", 1), ("S2", 5),
+    ("M", 2), ("AE", 4, 1, "S"), ("AQ", 3, 2), ("DF", 10), ("Y", 4), ("AE", 3, 1, "S"),
+    ("Y", 5), ("AT", 4, 2), ("DR", 9, "S"), ("TP", 9), ("AQ", 3, 1), ("M", 4),
+    ("S2", 6), ("M", 5), ("EX", 4), ("S2", 7), ("U", 9), ("AE", 4, 2, "S"),
+    ("Y", 6), ("DF", 11), ("DR", 10, "S"), ("EX", 2), ("Y", 7), ("AT", 5, 0),
+    ("DR", 11, "S"), ("M", 6), ("TP", 10), ("EX", 5), ("TP", 11), ("AQ", 4, 0),
+    ("AT", 5, 2), ("EX", 6), ("M", 7), ("AT", 5, 1), ("AQ", 4, 1), ("AE", 5, 0, "S"),
+    ("AQ", 4, 2), ("U", 10), ("AE", 5, 2, "S"), ("S2", 8), ("EX", 7), ("U", 11),
+    ("S2", 9), ("AQ", 5, 2), ("AE", 5, 1, "S"), ("AQ", 5, 0), ("LN", 0, 8), ("Y", 8),
+    ("AQ", 5, 1), ("M", 8), ("S2", 10), ("Y", 9), ("EX", 8), ("S2", 11),
+    ("SH", 0, 8), ("Y", 10), ("FN", 0, "G"), ("M", 9), ("FN", 1, "G"), ("Y", 11),
+    ("FN", 2, "G"), ("M", 10), ("EX", 9), ("M", 11), ("FN", 3, "G"), ("EX", 10),
+    ("EX", 11), ("FN", 4, "G"), ("FN", 5, "G"), ("LN", 8, 12), ("FN", 6, "G"), ("FN", 7, "G"),
+    ("SH", 8, 12), ("FN", 9, "S"), ("FN", 8, "V"), ("FN", 10, "G"), ("FN", 11, "G"),
 )
 
 
@@ -67,9 +67,7 @@ def tile_gcn_pc_kernel(tc, x_gc2, adj1, W3, b3, out):
         keep = ctx.enter_context(tc.tile_pool(name="keep", bufs=1))
         grp_pool = ctx.enter_context(tc.tile_pool(name="grp", bufs=9))
         junk = ctx.enter_context(tc.tile_pool(name="junk", bufs=2))
-        ps_tr = ctx.enter_context(tc.psum_pool(name="pstr", bufs=3))
-        ps_acc = ctx.enter_context(tc.psum_pool(name="psacc", bufs=4))
-        ps_deg = ctx.enter_context(tc.psum_pool(name="psdeg", bufs=1))
+        psum = ctx.enter_context(tc.psum_pool(name="psum", bufs=8))
 
         x_v = x_gc2.rearrange("(a m e) k -> m a (e k)", a=NPAIR, m=P, e=2)
         adj_v = adj1.rearrange("(a m e) j -> m a (e j)", a=NPAIR, m=P, e=2)
@@ -91,15 +89,13 @@ def tile_gcn_pc_kernel(tc, x_gc2, adj1, W3, b3, out):
         adjq = [keep.tile([P, NG * 256], U32, name="adjq%d" % a, align_bytes=64) for a in range(NPAIR)]
         adjs = [keep.tile([P, NG * 256], U8, name="adjs%d" % a, align_bytes=64) for a in range(NPAIR)]
         y_sb = [keep.tile([P, H], F32, name="y_sb%d" % n) for n in range(NT)]
-        part_sb = [keep.tile([P, 8 * RP], F32, name="part_sb%d" % r) for r in range(NPAIR // RP)]
-        deg_sb = [keep.tile([P, 2 * RP], F32, name="deg_sb%d" % r) for r in range(NPAIR // RP)]
-        fold = keep.tile([P, 32], F32, name="fold")
-        sel = keep.tile([P, 640], F32, name="sel")
+        deg = [keep.tile([P, 1], F32, name="deg%d" % n) for n in range(NT)]
         negm = keep.tile([P, NT], F32, name="negm")
         sums = keep.tile([P, NT], F32, name="sums")
         lns = keep.tile([P, NT], F32, name="lns")
         shift = keep.tile([P, NT], F32, name="shift")
         ident = keep.tile([P, P], F32, name="ident")
+        ident_bf = keep.tile([P, P], BF16, name="ident_bf")
         ones = keep.tile([P, P], BF16, name="ones")
         b3row = keep.tile([P, H], BF16, name="b3row")
         b3bc = keep.tile([P, H], F32, name="b3bc")
@@ -114,6 +110,11 @@ def tile_gcn_pc_kernel(tc, x_gc2, adj1, W3, b3, out):
             else:
                 nc.scalar.copy(out=dst, in_=src)
 
+        def new_bank(key):
+            bank = psum.tile([P, H], F32, name="bank")
+            banks[key] = bank
+            return bank
+
         def op_wr(w):
             nc.vector.tensor_copy(
                 out=w_grp[w][:].rearrange("p (c i t) -> p c t i", c=P, i=4, t=4),
@@ -125,8 +126,7 @@ def tile_gcn_pc_kernel(tc, x_gc2, adj1, W3, b3, out):
 
         def op_xt(g, b):
             words = x_sb[g][:].bitcast(F32)
-            bank = ps_tr.tile([P, H], F32, name="tr")
-            banks[("XT", g, b)] = bank
+            bank = new_bank(("XT", g, b))
             for n2 in range(2):
                 for h in range(2):
                     col = (2 * b + n2) * 256 + h * P
@@ -143,8 +143,7 @@ def tile_gcn_pc_kernel(tc, x_gc2, adj1, W3, b3, out):
             nc.vector.quantize_mx(out=xq[g][:].bitcast(FP8X4), scales=xs[g][:], in_=x_grp[g][:])
 
         def op_bp(g, cs):
-            bank = ps_acc.tile([P, H], F32, name="acc")
-            banks[("BP", g, cs)] = bank
+            bank = new_bank(("BP", g, cs))
             for t in range(4):
                 nc.tensor.matmul_mx(
                     out=bank[:, t * P : (t + 1) * P],
@@ -167,17 +166,14 @@ def tile_gcn_pc_kernel(tc, x_gc2, adj1, W3, b3, out):
             nc.vector.quantize_mx(out=botq[g][:].bitcast(FP8X4), scales=bots[g][:], in_=bot_grp[g][:])
 
         def op_b3():
-            bank = ps_tr.tile([P, H], F32, name="tr")
-            banks[("B3",)] = bank
-            nc.tensor.matmul(out=bank[:], lhsT=ones[:], rhs=b3row[:], start=True, stop=True)
+            nc.tensor.matmul(out=new_bank(("B3",))[:], lhsT=ones[:], rhs=b3row[:], start=True, stop=True)
 
         def op_b3c(eng):
             copy_on(eng, b3bc[:], banks[("B3",)][:])
 
         def op_at(a, g):
             words = adj_sb[a][:].bitcast(F32)
-            bank = ps_tr.tile([P, H], F32, name="tr")
-            banks[("AT", a, g)] = bank
+            bank = new_bank(("AT", a, g))
             for e in range(2):
                 for u in range(2):
                     col = e * 768 + g * 256 + u * P
@@ -199,44 +195,38 @@ def tile_gcn_pc_kernel(tc, x_gc2, adj1, W3, b3, out):
                 in_=grouped[(a, g)][:],
             )
 
-        def op_dg(a):
-            r = a // RP
-            if a % RP == 0:
-                banks[("PART", r)] = ps_deg.tile([P, H], F32, name="part")
-            part = banks[("PART", r)]
-            for e in range(2):
-                nl = 2 * (a % RP) + e
-                for s in range(4):
-                    col = 2 * RP * s + nl
-                    for g in range(NG):
-                        nc.tensor.matmul(
-                            out=part[:, col : col + 1],
-                            lhsT=grouped[(a, g)][:, e * H + s * P : e * H + (s + 1) * P],
-                            rhs=ones[:, 0:1],
-                            start=(g == 0),
-                            stop=(g == NG - 1),
-                        )
+        def op_dv(n, eng):
+            rows = adj_sb[n // 2][:, (n % 2) * NODES : (n % 2 + 1) * NODES]
+            dj = junk.tile([P, NODES], BF16, name="dj")
+            if eng == "V":
+                nc.vector.tensor_scalar(
+                    out=dj[:], in0=rows, scalar1=1.0, scalar2=None, op0=ALU.mult, op1=ALU.add, accum_out=deg[n][:]
+                )
+            else:
+                nc.scalar.activation(out=dj[:], in_=rows, func=ACT.Copy, accum_out=deg[n][:])
 
-        def op_slc(r, eng):
-            copy_on(eng, part_sb[r][:], banks[("PART", r)][:, 0 : 8 * RP])
-
-        def op_slm(r):
-            for s in range(4):
+        def op_df(n):
+            bank = new_bank(("DF", n))
+            base = (n % 2) * NODES
+            for r in range(NODES // P):
                 nc.tensor.matmul(
-                    out=banks[("PART", r)][:, 256 : 256 + 2 * RP],
-                    lhsT=sel[:, s * P : (s + 1) * P],
-                    rhs=part_sb[r][:, 2 * RP * s : 2 * RP * (s + 1)],
-                    start=(s == 0),
-                    stop=(s == 3),
+                    out=bank[:, 0:P],
+                    lhsT=ident_bf[:],
+                    rhs=adj_sb[n // 2][:, base + r * P : base + (r + 1) * P],
+                    start=(r == 0),
+                    stop=(r == NODES // P - 1),
                 )
 
-        def op_sld(r, eng):
-            copy_on(eng, deg_sb[r][:], banks[("PART", r)][:, 256 : 256 + 2 * RP])
+        def op_dr(n, eng):
+            if eng == "V":
+                nc.vector.tensor_reduce(out=deg[n][:], in_=banks[("DF", n)][:, 0:P], axis=AX.X, op=ALU.add)
+            else:
+                fj = junk.tile([P, P], F32, name="fj")
+                nc.scalar.activation(out=fj[:], in_=banks[("DF", n)][:, 0:P], func=ACT.Copy, accum_out=deg[n][:])
 
         def op_s2(n):
             a, e = n // 2, n % 2
-            bank = ps_acc.tile([P, H], F32, name="acc")
-            banks[("S2", n)] = bank
+            bank = new_bank(("S2", n))
             for g in range(NG):
                 col = g * 256 + e * P
                 nc.tensor.matmul_mx(
@@ -249,15 +239,10 @@ def tile_gcn_pc_kernel(tc, x_gc2, adj1, W3, b3, out):
                     stop=(g == NG - 1),
                 )
 
-        def op_u(n):
-            nc.vector.tensor_tensor(out=y_sb[n][:], in0=banks[("S2", n)][:], in1=b3bc[:], op=ALU.add)
-
         def op_tp(n):
             g0, t0 = n // 4, n % 4
-            bank = ps_acc.tile([P, H], F32, name="acc")
-            banks[("TP", n)] = bank
             nc.tensor.matmul_mx(
-                out=bank[:],
+                out=new_bank(("TP", n))[:],
                 lhsT=xq[g0][:, t0 * P : (t0 + 1) * P].bitcast(FP8X4),
                 lhsT_scale=xs[g0][:, t0 * P : (t0 + 1) * P],
                 rhs=wq[0][:].bitcast(FP8X4),
@@ -266,12 +251,13 @@ def tile_gcn_pc_kernel(tc, x_gc2, adj1, W3, b3, out):
                 stop=True,
             )
 
-        def op_y(n):
-            r, nl = n // (2 * RP), n % (2 * RP)
+        def op_u(n):
             nc.vector.scalar_tensor_tensor(
-                out=y_sb[n][:], in0=banks[("TP", n)][:], scalar=deg_sb[r][:, nl : nl + 1], in1=y_sb[n][:],
-                op0=ALU.mult, op1=ALU.add,
+                out=y_sb[n][:], in0=banks[("TP", n)][:], scalar=deg[n][:], in1=b3bc[:], op0=ALU.mult, op1=ALU.add
             )
+
+        def op_y(n):
+            nc.vector.tensor_tensor(out=y_sb[n][:], in0=banks[("S2", n)][:], in1=y_sb[n][:], op=ALU.add)
 
         def op_m(n):
             nc.vector.tensor_reduce(out=negm[:, n : n + 1], in_=y_sb[n][:], axis=AX.X, op=ALU.max, negate=True)
@@ -301,9 +287,8 @@ def tile_gcn_pc_kernel(tc, x_gc2, adj1, W3, b3, out):
 
         ops = {
             "WR": op_wr, "WQ": op_wq, "XT": op_xt, "XE": op_xe, "XQ": op_xq, "BP": op_bp, "BE": op_be, "BQ": op_bq,
-            "B3": op_b3, "B3C": op_b3c, "AT": op_at, "AE": op_ae, "AQ": op_aq, "DG": op_dg, "SLC": op_slc,
-            "SLM": op_slm, "SLD": op_sld, "S2": op_s2, "U": op_u, "TP": op_tp, "Y": op_y, "M": op_m, "EX": op_ex,
-            "LN": op_ln, "SH": op_sh, "FN": op_fn,
+            "B3": op_b3, "B3C": op_b3c, "AT": op_at, "AE": op_ae, "AQ": op_aq, "DV": op_dv, "DF": op_df, "DR": op_dr,
+            "S2": op_s2, "U": op_u, "TP": op_tp, "Y": op_y, "M": op_m, "EX": op_ex, "LN": op_ln, "SH": op_sh, "FN": op_fn,
         }
 
         with tc.manual_schedule():
@@ -322,13 +307,6 @@ def tile_gcn_pc_kernel(tc, x_gc2, adj1, W3, b3, out):
             nc.scalar.activation(out=warm[:, 1:2], in_=warm[:, 0:1], func=ACT.Exp)
             make_identity(nc, ident[:])
             nc.vector.memset(ones[:], 1.0)
-            nc.vector.memset(sel[:], 0.0)
-            nc.vector.tensor_reduce(
-                out=fold[:], in_=ident[:].rearrange("q (r t) -> q r t", r=32, t=4), axis=AX.X, op=ALU.add
-            )
-            nc.vector.tensor_copy(
-                out=sel[:].rearrange("q (s w) -> q s w", s=4, w=160)[:, :, 0:32],
-                in_=fold[:].unsqueeze(1).to_broadcast([P, 4, 32]),
-            )
+            nc.vector.tensor_copy(out=ident_bf[:], in_=ident[:])
             for step in ORDER:
                 ops[step[0]](*step[1:])

@@ -17,296 +17,300 @@ AX = mybir.AxisListType
 P = 128
 H = 512
 NODES = 1536
-NG = 3
-NPAIR = 6
-NT = 12
-LOADS = (("x", 0), ("w", 1), ("x", 1), ("x", 2), ("w", 0), ("a", 0), ("a", 1), ("a", 2), ("a", 3), ("a", 4), ("a", 5))
+GROUPS = NODES // H
+PAIRS = NODES // (2 * P)
+TILES = 2 * PAIRS
+TOP = 0
+BOT = 1
 
-ORDER = (
-    ("XT", 0, 0), ("XT", 0, 1), ("XE", 0, 1, "S"), ("WR", 1), ("B3",), ("XE", 0, 0, "S"),
-    ("B3C", "S"), ("XT", 1, 1), ("XQ", 0), ("XT", 1, 0), ("WQ", 1), ("XE", 1, 0, "S"),
-    ("XT", 2, 0), ("BP", 0, 0), ("XE", 1, 1, "S"), ("XE", 2, 0, "V"), ("BP", 0, 3), ("BE", 0, 0, "S"),
-    ("BP", 0, 2), ("WR", 0), ("BP", 0, 1), ("BE", 0, 3, "S"), ("XT", 2, 1), ("BE", 0, 2, "S"),
-    ("XQ", 1), ("BE", 0, 1, "S"), ("AT", 0, 2), ("DV", 0, "V"), ("BP", 1, 0), ("XE", 2, 1, "S"),
-    ("BP", 1, 1), ("WQ", 0), ("BP", 1, 2), ("BE", 1, 1, "S"), ("BP", 1, 3), ("BQ", 0),
-    ("TP", 0), ("BE", 1, 0, "S"), ("AT", 0, 0), ("XQ", 2), ("BE", 1, 3, "S"), ("AT", 0, 1),
-    ("DV", 2, "V"), ("AT", 1, 2), ("BE", 1, 2, "S"), ("DF", 1), ("AE", 0, 0, "S"), ("DV", 4, "V"),
-    ("BP", 2, 1), ("AE", 0, 2, "S"), ("BP", 2, 0), ("BQ", 1), ("BP", 2, 2), ("AE", 0, 1, "S"),
-    ("TP", 1), ("DR", 1, "V"), ("BE", 2, 0, "S"), ("BP", 2, 3), ("U", 0), ("AT", 1, 1),
-    ("BE", 2, 2, "S"), ("AQ", 0, 0), ("DF", 3), ("AQ", 0, 1), ("BE", 2, 3, "S"), ("DV", 6, "V"),
-    ("BE", 2, 1, "S"), ("TP", 2), ("AT", 1, 0), ("U", 1), ("AE", 1, 1, "S"), ("DF", 5),
-    ("BQ", 2), ("DR", 3, "S"), ("AE", 1, 2, "S"), ("TP", 7), ("AQ", 0, 2), ("TP", 3),
-    ("AE", 1, 0, "S"), ("U", 2), ("S2", 0), ("DV", 8, "S"), ("DR", 5, "V"), ("AQ", 1, 2),
-    ("TP", 4), ("AQ", 1, 1), ("S2", 1), ("AQ", 1, 0), ("U", 3), ("S2", 2),
-    ("Y", 0), ("U", 4), ("S2", 3), ("Y", 1), ("TP", 6), ("Y", 2),
-    ("AT", 2, 2), ("AT", 2, 0), ("Y", 3), ("AT", 3, 2), ("AE", 2, 0, "S"), ("M", 0),
-    ("AT", 2, 1), ("DF", 7), ("U", 6), ("AE", 2, 1, "S"), ("M", 1), ("AE", 2, 2, "S"),
-    ("TP", 5), ("TP", 8), ("AQ", 2, 1), ("AE", 3, 2, "S"), ("DF", 9), ("M", 3),
-    ("DR", 7, "S"), ("EX", 0), ("U", 8), ("AT", 3, 0), ("AT", 4, 0), ("AQ", 2, 0),
-    ("AE", 3, 0, "S"), ("AT", 4, 1), ("AQ", 2, 2), ("AT", 3, 1), ("U", 5), ("AE", 4, 0, "S"),
-    ("S2", 4), ("EX", 3), ("U", 7), ("AQ", 3, 0), ("EX", 1), ("S2", 5),
-    ("M", 2), ("AE", 4, 1, "S"), ("AQ", 3, 2), ("DF", 10), ("Y", 4), ("AE", 3, 1, "S"),
-    ("Y", 5), ("AT", 4, 2), ("DR", 9, "S"), ("TP", 9), ("AQ", 3, 1), ("M", 4),
-    ("S2", 6), ("M", 5), ("EX", 4), ("S2", 7), ("U", 9), ("AE", 4, 2, "S"),
-    ("Y", 6), ("DF", 11), ("DR", 10, "S"), ("EX", 2), ("Y", 7), ("AT", 5, 0),
-    ("DR", 11, "S"), ("M", 6), ("TP", 10), ("EX", 5), ("TP", 11), ("AQ", 4, 0),
-    ("AT", 5, 2), ("EX", 6), ("M", 7), ("AT", 5, 1), ("AQ", 4, 1), ("AE", 5, 0, "S"),
-    ("AQ", 4, 2), ("U", 10), ("AE", 5, 2, "S"), ("S2", 8), ("EX", 7), ("U", 11),
-    ("S2", 9), ("AQ", 5, 2), ("AE", 5, 1, "S"), ("AQ", 5, 0), ("LN", 0, 8), ("Y", 8),
-    ("AQ", 5, 1), ("M", 8), ("S2", 10), ("Y", 9), ("EX", 8), ("S2", 11),
-    ("SH", 0, 8), ("Y", 10), ("FN", 0, "G"), ("M", 9), ("FN", 1, "G"), ("Y", 11),
-    ("FN", 2, "G"), ("M", 10), ("EX", 9), ("M", 11), ("FN", 3, "G"), ("EX", 10),
-    ("EX", 11), ("FN", 4, "G"), ("FN", 5, "G"), ("LN", 8, 12), ("FN", 6, "G"), ("FN", 7, "G"),
-    ("SH", 8, 12), ("FN", 9, "S"), ("FN", 8, "V"), ("FN", 10, "G"), ("FN", 11, "G"),
-)
+DEG_ON_TENSOR = (1, 3, 5, 7, 9, 10, 11)
+DEG_ON_SCALAR = (6, 8)
+BOT_COPY_ON_VECTOR = (0, 3)
+LAG = 2
+FIRST_LOG = 8
 
 
 def tile_gcn_pc_kernel(tc, x_gc2, adj1, W3, b3, out):
     nc = tc.nc
     with ExitStack() as ctx:
         keep = ctx.enter_context(tc.tile_pool(name="keep", bufs=1))
-        grp_pool = ctx.enter_context(tc.tile_pool(name="grp", bufs=9))
-        junk = ctx.enter_context(tc.tile_pool(name="junk", bufs=2))
+        regrouped = ctx.enter_context(tc.tile_pool(name="regrouped", bufs=9))
+        unread = ctx.enter_context(tc.tile_pool(name="unread", bufs=2))
         psum = ctx.enter_context(tc.psum_pool(name="psum", bufs=8))
 
-        x_v = x_gc2.rearrange("(a m e) k -> m a (e k)", a=NPAIR, m=P, e=2)
-        adj_v = adj1.rearrange("(a m e) j -> m a (e j)", a=NPAIR, m=P, e=2)
-        w_v = W3.rearrange("(w h q e) c -> q w h (e c)", w=2, h=2, q=P, e=2)
-        out_v = out.rearrange("(a m e) c -> m a (e c)", a=NPAIR, m=P, e=2)
+        x_v = x_gc2.rearrange("(a m e) k -> m a (e k)", a=PAIRS, m=P, e=2)
+        adj_v = adj1.rearrange("(a m e) j -> m a (e j)", a=PAIRS, m=P, e=2)
+        out_v = out.rearrange("(a m e) c -> m a (e c)", a=PAIRS, m=P, e=2)
+        w_v = W3.rearrange("(w u q e) c -> q w u (e c)", w=2, u=2, q=P, e=2)
 
-        w_raw = [keep.tile([P, 4 * H], BF16, name="w_raw%d" % w) for w in range(2)]
-        w_grp = [keep.tile([P, 4 * H], BF16, name="w_grp%d" % w, align_bytes=64) for w in range(2)]
-        wq = [keep.tile([P, H], U32, name="wq%d" % w, align_bytes=64) for w in range(2)]
-        ws = [keep.tile([P, H], U8, name="ws%d" % w, align_bytes=64) for w in range(2)]
-        x_sb = [keep.tile([P, 4 * H], BF16, name="x_sb%d" % g) for g in range(NG)]
-        x_grp = [keep.tile([P, 4 * H], BF16, name="x_grp%d" % g, align_bytes=64) for g in range(NG)]
-        xq = [keep.tile([P, H], U32, name="xq%d" % g, align_bytes=64) for g in range(NG)]
-        xs = [keep.tile([P, H], U8, name="xs%d" % g, align_bytes=64) for g in range(NG)]
-        bot_grp = [keep.tile([P, 4 * H], BF16, name="bot_grp%d" % g, align_bytes=64) for g in range(NG)]
-        botq = [keep.tile([P, H], U32, name="botq%d" % g, align_bytes=64) for g in range(NG)]
-        bots = [keep.tile([P, H], U8, name="bots%d" % g, align_bytes=64) for g in range(NG)]
-        adj_sb = [keep.tile([P, 2 * NODES], BF16, name="adj_sb%d" % a) for a in range(NPAIR)]
-        adjq = [keep.tile([P, NG * 256], U32, name="adjq%d" % a, align_bytes=64) for a in range(NPAIR)]
-        adjs = [keep.tile([P, NG * 256], U8, name="adjs%d" % a, align_bytes=64) for a in range(NPAIR)]
-        y_sb = [keep.tile([P, H], F32, name="y_sb%d" % n) for n in range(NT)]
-        deg = [keep.tile([P, 1], F32, name="deg%d" % n) for n in range(NT)]
-        negm = keep.tile([P, NT], F32, name="negm")
-        sums = keep.tile([P, NT], F32, name="sums")
-        lns = keep.tile([P, NT], F32, name="lns")
-        shift = keep.tile([P, NT], F32, name="shift")
+        w_rows = [keep.tile([P, 4 * H], BF16, name="w_rows%d" % w) for w in range(2)]
+        w_words = [keep.tile([P, 4 * H], BF16, name="w_words%d" % w, align_bytes=64) for w in range(2)]
+        w_codes = [keep.tile([P, H], U32, name="w_codes%d" % w, align_bytes=64) for w in range(2)]
+        w_scales = [keep.tile([P, H], U8, name="w_scales%d" % w, align_bytes=64) for w in range(2)]
+        x_rows = [keep.tile([P, 4 * H], BF16, name="x_rows%d" % g) for g in range(GROUPS)]
+        x_words = [keep.tile([P, 4 * H], BF16, name="x_words%d" % g, align_bytes=64) for g in range(GROUPS)]
+        x_codes = [keep.tile([P, H], U32, name="x_codes%d" % g, align_bytes=64) for g in range(GROUPS)]
+        x_scales = [keep.tile([P, H], U8, name="x_scales%d" % g, align_bytes=64) for g in range(GROUPS)]
+        bot_words = [keep.tile([P, 4 * H], BF16, name="bot_words%d" % g, align_bytes=64) for g in range(GROUPS)]
+        bot_codes = [keep.tile([P, H], U32, name="bot_codes%d" % g, align_bytes=64) for g in range(GROUPS)]
+        bot_scales = [keep.tile([P, H], U8, name="bot_scales%d" % g, align_bytes=64) for g in range(GROUPS)]
+        adj_rows = [keep.tile([P, 2 * NODES], BF16, name="adj_rows%d" % a) for a in range(PAIRS)]
+        adj_codes = [keep.tile([P, GROUPS * 2 * P], U32, name="adj_codes%d" % a, align_bytes=64) for a in range(PAIRS)]
+        adj_scales = [keep.tile([P, GROUPS * 2 * P], U8, name="adj_scales%d" % a, align_bytes=64) for a in range(PAIRS)]
+        y = [keep.tile([P, H], F32, name="y%d" % n) for n in range(TILES)]
+        deg = [keep.tile([P, 1], F32, name="deg%d" % n) for n in range(TILES)]
+        neg_max = keep.tile([P, TILES], F32, name="neg_max")
+        exp_sum = keep.tile([P, TILES], F32, name="exp_sum")
+        log_sum = keep.tile([P, TILES], F32, name="log_sum")
+        shift = keep.tile([P, TILES], F32, name="shift")
         ident = keep.tile([P, P], F32, name="ident")
         ident_bf = keep.tile([P, P], BF16, name="ident_bf")
         ones = keep.tile([P, P], BF16, name="ones")
-        b3row = keep.tile([P, H], BF16, name="b3row")
-        b3bc = keep.tile([P, H], F32, name="b3bc")
+        b3_row = keep.tile([P, H], BF16, name="b3_row")
+        b3_all = keep.tile([P, H], F32, name="b3_all")
         warm = keep.tile([P, 2], F32, name="warm")
 
-        banks = {}
-        grouped = {}
+        x_ps, bot_ps, adj_ps, adj_words, fold_ps, top_ps, ab_ps, b3_ps = {}, {}, {}, {}, {}, {}, {}, {}
 
-        def copy_on(eng, dst, src):
-            if eng == "V":
-                nc.vector.tensor_copy(out=dst, in_=src)
-            else:
-                nc.scalar.copy(out=dst, in_=src)
+        def bank():
+            return psum.tile([P, H], F32, name="bank")
 
-        def new_bank(key):
-            bank = psum.tile([P, H], F32, name="bank")
-            banks[key] = bank
-            return bank
+        def tiles_of(a):
+            return (2 * a, 2 * a + 1)
 
-        def op_wr(w):
-            nc.vector.tensor_copy(
-                out=w_grp[w][:].rearrange("p (c i t) -> p c t i", c=P, i=4, t=4),
-                in_=w_raw[w][:].rearrange("p (t c i) -> p c t i", t=4, c=P, i=4),
-            )
+        def rows_of(n):
+            return adj_rows[n // 2][:, (n % 2) * NODES : (n % 2 + 1) * NODES]
 
-        def op_wq(w):
-            nc.vector.quantize_mx(out=wq[w][:].bitcast(FP8X4), scales=ws[w][:], in_=w_grp[w][:])
+        def transpose_words(dst, words, columns):
+            for i, col in enumerate(columns):
+                nc.tensor.transpose(dst[:, i * P : (i + 1) * P], words[:, col : col + P], ident[:])
 
-        def op_xt(g, b):
-            words = x_sb[g][:].bitcast(F32)
-            bank = new_bank(("XT", g, b))
-            for n2 in range(2):
-                for h in range(2):
-                    col = (2 * b + n2) * 256 + h * P
-                    nc.tensor.transpose(bank[:, (2 * n2 + h) * P : (2 * n2 + h + 1) * P], words[:, col : col + P], ident[:])
+        def x_transposes(g):
+            for b in range(2):
+                x_ps[g, b] = bank()
+                transpose_words(x_ps[g, b], x_rows[g][:].bitcast(F32), [(4 * b + i) * P for i in range(4)])
 
-        def op_xe(g, b, eng):
-            copy_on(
-                eng,
-                x_grp[g][:].bitcast(F32)[:, b * H : (b + 1) * H].rearrange("q (n r h) -> q n r h", n=2, r=P, h=2),
-                banks[("XT", g, b)][:].rearrange("q (n h r) -> q n r h", n=2, h=2, r=P),
-            )
-
-        def op_xq(g):
-            nc.vector.quantize_mx(out=xq[g][:].bitcast(FP8X4), scales=xs[g][:], in_=x_grp[g][:])
-
-        def op_bp(g, cs):
-            bank = new_bank(("BP", g, cs))
-            for t in range(4):
-                nc.tensor.matmul_mx(
-                    out=bank[:, t * P : (t + 1) * P],
-                    lhsT=xq[g][:, t * P : (t + 1) * P].bitcast(FP8X4),
-                    lhsT_scale=xs[g][:, t * P : (t + 1) * P],
-                    rhs=wq[1][:, cs * P : (cs + 1) * P].bitcast(FP8X4),
-                    rhs_scale=ws[1][:, cs * P : (cs + 1) * P],
-                    start=True,
-                    stop=True,
+        def adj_transposes(a):
+            for g in range(GROUPS):
+                adj_ps[a, g] = bank()
+                transpose_words(
+                    adj_ps[a, g], adj_rows[a][:].bitcast(F32), [e * (NODES // 2) + (2 * g + u) * P for e in range(2) for u in range(2)]
                 )
 
-        def op_be(g, cs, eng):
-            copy_on(
-                eng,
-                bot_grp[g][:, cs * H : (cs + 1) * H].rearrange("m (c t) -> m c t", c=P, t=4),
-                banks[("BP", g, cs)][:].rearrange("m (t c) -> m c t", t=4, c=P),
-            )
-
-        def op_bq(g):
-            nc.vector.quantize_mx(out=botq[g][:].bitcast(FP8X4), scales=bots[g][:], in_=bot_grp[g][:])
-
-        def op_b3():
-            nc.tensor.matmul(out=new_bank(("B3",))[:], lhsT=ones[:], rhs=b3row[:], start=True, stop=True)
-
-        def op_b3c(eng):
-            copy_on(eng, b3bc[:], banks[("B3",)][:])
-
-        def op_at(a, g):
-            words = adj_sb[a][:].bitcast(F32)
-            bank = new_bank(("AT", a, g))
-            for e in range(2):
-                for u in range(2):
-                    col = e * 768 + g * 256 + u * P
-                    nc.tensor.transpose(bank[:, (2 * e + u) * P : (2 * e + u + 1) * P], words[:, col : col + P], ident[:])
-
-        def op_ae(a, g, eng):
-            agrp = grp_pool.tile([P, 2 * H], BF16, name="agrp", align_bytes=64)
-            grouped[(a, g)] = agrp
-            copy_on(
-                eng,
-                agrp[:].bitcast(F32).rearrange("q (e i u) -> q e i u", e=2, i=P, u=2),
-                banks[("AT", a, g)][:].rearrange("q (e u i) -> q e i u", e=2, u=2, i=P),
-            )
-
-        def op_aq(a, g):
-            nc.vector.quantize_mx(
-                out=adjq[a][:, g * 256 : (g + 1) * 256].bitcast(FP8X4),
-                scales=adjs[a][:, g * 256 : (g + 1) * 256],
-                in_=grouped[(a, g)][:],
-            )
-
-        def op_dv(n, eng):
-            rows = adj_sb[n // 2][:, (n % 2) * NODES : (n % 2 + 1) * NODES]
-            dj = junk.tile([P, NODES], BF16, name="dj")
-            if eng == "V":
-                nc.vector.tensor_scalar(
-                    out=dj[:], in0=rows, scalar1=1.0, scalar2=None, op0=ALU.mult, op1=ALU.add, accum_out=deg[n][:]
-                )
-            else:
-                nc.scalar.activation(out=dj[:], in_=rows, func=ACT.Copy, accum_out=deg[n][:])
-
-        def op_df(n):
-            bank = new_bank(("DF", n))
-            base = (n % 2) * NODES
-            for r in range(NODES // P):
-                nc.tensor.matmul(
-                    out=bank[:, 0:P],
-                    lhsT=ident_bf[:],
-                    rhs=adj_sb[n // 2][:, base + r * P : base + (r + 1) * P],
-                    start=(r == 0),
-                    stop=(r == NODES // P - 1),
-                )
-
-        def op_dr(n, eng):
-            if eng == "V":
-                nc.vector.tensor_reduce(out=deg[n][:], in_=banks[("DF", n)][:, 0:P], axis=AX.X, op=ALU.add)
-            else:
-                fj = junk.tile([P, P], F32, name="fj")
-                nc.scalar.activation(out=fj[:], in_=banks[("DF", n)][:, 0:P], func=ACT.Copy, accum_out=deg[n][:])
-
-        def op_s2(n):
-            a, e = n // 2, n % 2
-            bank = new_bank(("S2", n))
-            for g in range(NG):
-                col = g * 256 + e * P
-                nc.tensor.matmul_mx(
-                    out=bank[:],
-                    lhsT=adjq[a][:, col : col + P].bitcast(FP8X4),
-                    lhsT_scale=adjs[a][:, col : col + P],
-                    rhs=botq[g][:].bitcast(FP8X4),
-                    rhs_scale=bots[g][:],
-                    start=(g == 0),
-                    stop=(g == NG - 1),
-                )
-
-        def op_tp(n):
-            g0, t0 = n // 4, n % 4
+        def mx_pass(dst, lhs_codes, lhs_scales, lhs_cols, rhs_codes, rhs_scales, rhs_cols, start, stop):
             nc.tensor.matmul_mx(
-                out=new_bank(("TP", n))[:],
-                lhsT=xq[g0][:, t0 * P : (t0 + 1) * P].bitcast(FP8X4),
-                lhsT_scale=xs[g0][:, t0 * P : (t0 + 1) * P],
-                rhs=wq[0][:].bitcast(FP8X4),
-                rhs_scale=ws[0][:],
-                start=True,
-                stop=True,
+                out=dst,
+                lhsT=lhs_codes[:, lhs_cols].bitcast(FP8X4),
+                lhsT_scale=lhs_scales[:, lhs_cols],
+                rhs=rhs_codes[:, rhs_cols].bitcast(FP8X4),
+                rhs_scale=rhs_scales[:, rhs_cols],
+                start=start,
+                stop=stop,
             )
 
-        def op_u(n):
-            nc.vector.scalar_tensor_tensor(
-                out=y_sb[n][:], in0=banks[("TP", n)][:], scalar=deg[n][:], in1=b3bc[:], op0=ALU.mult, op1=ALU.add
+        def bot_passes(g):
+            for c in range(4):
+                bot_ps[g, c] = bank()
+                for t in range(4):
+                    mx_pass(
+                        bot_ps[g, c][:, t * P : (t + 1) * P],
+                        x_codes[g], x_scales[g], slice(t * P, (t + 1) * P),
+                        w_codes[BOT], w_scales[BOT], slice(c * P, (c + 1) * P),
+                        True, True,
+                    )
+
+        def top_pass(n):
+            top_ps[n] = bank()
+            mx_pass(
+                top_ps[n][:],
+                x_codes[n // 4], x_scales[n // 4], slice((n % 4) * P, (n % 4 + 1) * P),
+                w_codes[TOP], w_scales[TOP], slice(0, H),
+                True, True,
             )
 
-        def op_y(n):
-            nc.vector.tensor_tensor(out=y_sb[n][:], in0=banks[("S2", n)][:], in1=y_sb[n][:], op=ALU.add)
+        def second_product(n):
+            ab_ps[n] = bank()
+            for g in range(GROUPS):
+                col = (2 * g + n % 2) * P
+                mx_pass(
+                    ab_ps[n][:],
+                    adj_codes[n // 2], adj_scales[n // 2], slice(col, col + P),
+                    bot_codes[g], bot_scales[g], slice(0, H),
+                    g == 0, g == GROUPS - 1,
+                )
 
-        def op_m(n):
-            nc.vector.tensor_reduce(out=negm[:, n : n + 1], in_=y_sb[n][:], axis=AX.X, op=ALU.max, negate=True)
+        def fold_rows(a):
+            for n in tiles_of(a):
+                if n in DEG_ON_TENSOR:
+                    fold_ps[n] = bank()
+                    for r in range(NODES // P):
+                        nc.tensor.matmul(
+                            out=fold_ps[n][:, 0:P], lhsT=ident_bf[:], rhs=rows_of(n)[:, r * P : (r + 1) * P],
+                            start=(r == 0), stop=(r == NODES // P - 1),
+                        )
 
-        def op_ex(n):
-            ej = junk.tile([P, H], BF16, name="ej")
-            nc.scalar.activation(
-                out=ej[:], in_=y_sb[n][:], func=ACT.Exp, bias=negm[:, n : n + 1], scale=1.0,
-                accum_out=sums[:, n : n + 1],
+        def x_copies(g):
+            for b in range(2):
+                nc.scalar.copy(
+                    out=x_words[g][:].bitcast(F32)[:, b * H : (b + 1) * H].rearrange("q (n r u) -> q n r u", n=2, r=P, u=2),
+                    in_=x_ps[g, b][:].rearrange("q (n u r) -> q n r u", n=2, u=2, r=P),
+                )
+
+        def adj_copies(a):
+            for g in range(GROUPS):
+                adj_words[a, g] = regrouped.tile([P, 2 * H], BF16, name="adj_words", align_bytes=64)
+                nc.scalar.copy(
+                    out=adj_words[a, g][:].bitcast(F32).rearrange("q (e i u) -> q e i u", e=2, i=P, u=2),
+                    in_=adj_ps[a, g][:].rearrange("q (e u i) -> q e i u", e=2, u=2, i=P),
+                )
+
+        def bot_copies(g):
+            for c in range(4):
+                dst = bot_words[g][:, c * H : (c + 1) * H].rearrange("m (c t) -> m c t", c=P, t=4)
+                src = bot_ps[g, c][:].rearrange("m (t c) -> m c t", t=4, c=P)
+                if (g, c) == BOT_COPY_ON_VECTOR:
+                    nc.vector.tensor_copy(out=dst, in_=src)
+                else:
+                    nc.scalar.copy(out=dst, in_=src)
+
+        def folded_sums(a):
+            for n in tiles_of(a):
+                if n in DEG_ON_TENSOR:
+                    copied = unread.tile([P, P], F32, name="copied")
+                    nc.scalar.activation(out=copied[:], in_=fold_ps[n][:, 0:P], func=ACT.Copy, accum_out=deg[n][:])
+
+        def direct_sums(a):
+            for n in tiles_of(a):
+                if n not in DEG_ON_TENSOR:
+                    copied = unread.tile([P, NODES], BF16, name="rows_copied")
+                    if n in DEG_ON_SCALAR:
+                        nc.scalar.activation(out=copied[:], in_=rows_of(n), func=ACT.Copy, accum_out=deg[n][:])
+                    else:
+                        nc.vector.tensor_scalar(
+                            out=copied[:], in0=rows_of(n), scalar1=1.0, scalar2=None, op0=ALU.mult, op1=ALU.add,
+                            accum_out=deg[n][:],
+                        )
+
+        def regroup_w(w):
+            nc.vector.tensor_copy(
+                out=w_words[w][:].rearrange("p (c i t) -> p c t i", c=P, i=4, t=4),
+                in_=w_rows[w][:].rearrange("p (t c i) -> p c t i", t=4, c=P, i=4),
             )
 
-        def op_ln(lo, hi):
-            nc.scalar.activation(out=lns[:, lo:hi], in_=sums[:, lo:hi], func=ACT.Ln)
+        def quantise(codes, scales, words):
+            nc.vector.quantize_mx(out=codes.bitcast(FP8X4), scales=scales, in_=words)
 
-        def op_sh(lo, hi):
-            nc.vector.tensor_tensor(out=shift[:, lo:hi], in0=negm[:, lo:hi], in1=lns[:, lo:hi], op=ALU.subtract)
+        def quantise_adj(a):
+            for g in range(GROUPS):
+                cols = slice(g * 2 * P, (g + 1) * 2 * P)
+                quantise(adj_codes[a][:, cols], adj_scales[a][:, cols], adj_words[a, g][:])
 
-        def op_fn(n, eng):
-            y = y_sb[n][:]
-            if eng == "V":
-                nc.vector.tensor_scalar(out=y, in0=y, scalar1=shift[:, n : n + 1], scalar2=None, op0=ALU.add)
-            elif eng == "S":
-                nc.scalar.activation(out=y, in_=y, func=ACT.Identity, bias=shift[:, n : n + 1], scale=1.0)
-            else:
-                nc.gpsimd.tensor_scalar(out=y, in0=y, scalar1=1.0, scalar2=shift[:, n : n + 1], op0=ALU.mult, op1=ALU.add)
-            nc.sync.dma_start(out=out_v[:, n // 2, (n % 2) * H : (n % 2 + 1) * H], in_=y)
+        def scaled_top(a):
+            for n in tiles_of(a):
+                nc.vector.scalar_tensor_tensor(
+                    out=y[n][:], in0=top_ps[n][:], scalar=deg[n][:], in1=b3_all[:], op0=ALU.mult, op1=ALU.add
+                )
 
-        ops = {
-            "WR": op_wr, "WQ": op_wq, "XT": op_xt, "XE": op_xe, "XQ": op_xq, "BP": op_bp, "BE": op_be, "BQ": op_bq,
-            "B3": op_b3, "B3C": op_b3c, "AT": op_at, "AE": op_ae, "AQ": op_aq, "DV": op_dv, "DF": op_df, "DR": op_dr,
-            "S2": op_s2, "U": op_u, "TP": op_tp, "Y": op_y, "M": op_m, "EX": op_ex, "LN": op_ln, "SH": op_sh, "FN": op_fn,
-        }
+        def sums_and_maxima(a):
+            for n in tiles_of(a):
+                nc.vector.tensor_tensor(out=y[n][:], in0=ab_ps[n][:], in1=y[n][:], op=ALU.add)
+            for n in tiles_of(a):
+                nc.vector.tensor_reduce(out=neg_max[:, n : n + 1], in_=y[n][:], axis=AX.X, op=ALU.max, negate=True)
+
+        def exponentials(a):
+            for n in tiles_of(a):
+                powers = unread.tile([P, H], BF16, name="powers")
+                nc.scalar.activation(
+                    out=powers[:], in_=y[n][:], func=ACT.Exp, bias=neg_max[:, n : n + 1], scale=1.0,
+                    accum_out=exp_sum[:, n : n + 1],
+                )
+
+        def logarithms(lo, hi):
+            nc.scalar.activation(out=log_sum[:, lo:hi], in_=exp_sum[:, lo:hi], func=ACT.Ln)
+
+        def finish(lo, hi, in_a_hurry):
+            nc.vector.tensor_tensor(out=shift[:, lo:hi], in0=neg_max[:, lo:hi], in1=log_sum[:, lo:hi], op=ALU.subtract)
+            for n in range(lo, hi):
+                if not in_a_hurry:
+                    nc.gpsimd.tensor_scalar(
+                        out=y[n][:], in0=y[n][:], scalar1=1.0, scalar2=shift[:, n : n + 1], op0=ALU.mult, op1=ALU.add
+                    )
+                elif n % 2 == 0:
+                    nc.vector.tensor_scalar(out=y[n][:], in0=y[n][:], scalar1=shift[:, n : n + 1], scalar2=None, op0=ALU.add)
+                else:
+                    nc.scalar.activation(out=y[n][:], in_=y[n][:], func=ACT.Identity, bias=shift[:, n : n + 1], scale=1.0)
+                nc.sync.dma_start(out=out_v[:, n // 2, (n % 2) * H : (n % 2 + 1) * H], in_=y[n][:])
 
         with tc.manual_schedule():
-            nc.vector.memset(b3row[:], 0.0)
-            nc.scalar.dma_start(out=b3row[0:1, :], in_=b3.unsqueeze(0))
-            for kind, i in LOADS:
-                if kind == "x":
-                    nc.sync.dma_start(
-                        out=x_sb[i][:].rearrange("m (a f) -> m a f", a=2), in_=x_v[:, 2 * i : 2 * i + 2, :]
-                    )
-                elif kind == "w":
-                    nc.sync.dma_start(out=w_raw[i][:].rearrange("q (h f) -> q h f", h=2), in_=w_v[:, i])
-                else:
-                    nc.sync.dma_start(out=adj_sb[i][:], in_=adj_v[:, i, :])
+            nc.vector.memset(b3_row[:], 0.0)
+            nc.scalar.dma_start(out=b3_row[0:1, :], in_=b3.unsqueeze(0))
+            for g in range(GROUPS):
+                nc.sync.dma_start(out=x_rows[g][:].rearrange("m (a f) -> m a f", a=2), in_=x_v[:, 2 * g : 2 * g + 2, :])
+                if g == 0:
+                    nc.sync.dma_start(out=w_rows[BOT][:].rearrange("q (u f) -> q u f", u=2), in_=w_v[:, BOT])
+            nc.sync.dma_start(out=w_rows[TOP][:].rearrange("q (u f) -> q u f", u=2), in_=w_v[:, TOP])
+            for a in range(PAIRS):
+                nc.sync.dma_start(out=adj_rows[a][:], in_=adj_v[:, a, :])
             nc.vector.memset(warm[:], 0.0)
             nc.scalar.activation(out=warm[:, 1:2], in_=warm[:, 0:1], func=ACT.Exp)
             make_identity(nc, ident[:])
             nc.vector.memset(ones[:], 1.0)
             nc.vector.tensor_copy(out=ident_bf[:], in_=ident[:])
-            for step in ORDER:
-                ops[step[0]](*step[1:])
+
+            x_transposes(0)
+            x_copies(0)
+            regroup_w(BOT)
+            b3_ps[0] = bank()
+            nc.tensor.matmul(out=b3_ps[0][:], lhsT=ones[:], rhs=b3_row[:], start=True, stop=True)
+            nc.scalar.copy(out=b3_all[:], in_=b3_ps[0][:])
+            quantise(x_codes[0][:], x_scales[0][:], x_words[0][:])
+            x_transposes(1)
+            x_copies(1)
+            quantise(w_codes[BOT][:], w_scales[BOT][:], w_words[BOT][:])
+            quantise(x_codes[1][:], x_scales[1][:], x_words[1][:])
+            x_transposes(2)
+            x_copies(2)
+            regroup_w(TOP)
+            quantise(x_codes[2][:], x_scales[2][:], x_words[2][:])
+            bot_passes(0)
+            bot_copies(0)
+            bot_passes(1)
+            bot_copies(1)
+            direct_sums(0)
+            quantise(w_codes[TOP][:], w_scales[TOP][:], w_words[TOP][:])
+            quantise(bot_codes[0][:], bot_scales[0][:], bot_words[0][:])
+            fold_rows(0)
+
+            for j in range(PAIRS + LAG):
+                if j < PAIRS:
+                    adj_transposes(j)
+                if j >= LAG:
+                    for n in tiles_of(j - LAG):
+                        second_product(n)
+                if j < PAIRS:
+                    for n in tiles_of(j):
+                        top_pass(n)
+                    if j + 1 < PAIRS:
+                        fold_rows(j + 1)
+                    adj_copies(j)
+                    folded_sums(j)
+                    if j + 1 < PAIRS:
+                        direct_sums(j + 1)
+                if j == 0:
+                    bot_passes(2)
+                    bot_copies(2)
+                    quantise(bot_codes[1][:], bot_scales[1][:], bot_words[1][:])
+                if j == 1:
+                    quantise(bot_codes[2][:], bot_scales[2][:], bot_words[2][:])
+                if j >= LAG:
+                    sums_and_maxima(j - LAG)
+                    exponentials(j - LAG)
+                    if 2 * (j - LAG) + 2 == FIRST_LOG:
+                        logarithms(0, FIRST_LOG)
+                if j < PAIRS:
+                    quantise_adj(j)
+                    scaled_top(j)
+                if 2 * (j - LAG) == FIRST_LOG:
+                    finish(0, FIRST_LOG, False)
+            logarithms(FIRST_LOG, TILES)
+            finish(FIRST_LOG, TILES, True)

@@ -28,6 +28,7 @@ DEG_ON_SCALAR = (6, 8)
 BOT_COPY_ON_VECTOR = (0, 3)
 LAG = 2
 FIRST_LOG = 8
+FINISHED_BY_GPSIMD = 4
 
 
 def tile_gcn_pc_kernel(tc, x_gc2, adj1, W3, b3, out):
@@ -228,18 +229,24 @@ def tile_gcn_pc_kernel(tc, x_gc2, adj1, W3, b3, out):
         def logarithms(lo, hi):
             nc.scalar.activation(out=log_sum[:, lo:hi], in_=exp_sum[:, lo:hi], func=ACT.Ln)
 
-        def finish(lo, hi, in_a_hurry):
+        def store(n):
+            nc.sync.dma_start(out=out_v[:, n // 2, (n % 2) * H : (n % 2 + 1) * H], in_=y[n][:])
+
+        def finish_on_gpsimd(lo, hi):
             nc.vector.tensor_tensor(out=shift[:, lo:hi], in0=neg_max[:, lo:hi], in1=log_sum[:, lo:hi], op=ALU.subtract)
             for n in range(lo, hi):
-                if not in_a_hurry:
-                    nc.gpsimd.tensor_scalar(
-                        out=y[n][:], in0=y[n][:], scalar1=1.0, scalar2=shift[:, n : n + 1], op0=ALU.mult, op1=ALU.add
-                    )
-                elif n % 2 == 0:
-                    nc.vector.tensor_scalar(out=y[n][:], in0=y[n][:], scalar1=shift[:, n : n + 1], scalar2=None, op0=ALU.add)
-                else:
-                    nc.scalar.activation(out=y[n][:], in_=y[n][:], func=ACT.Identity, bias=shift[:, n : n + 1], scale=1.0)
-                nc.sync.dma_start(out=out_v[:, n // 2, (n % 2) * H : (n % 2 + 1) * H], in_=y[n][:])
+                nc.gpsimd.tensor_scalar(
+                    out=y[n][:], in0=y[n][:], scalar1=1.0, scalar2=shift[:, n : n + 1], op0=ALU.mult, op1=ALU.add
+                )
+                store(n)
+
+        def finish_on_vector(lo, hi):
+            for n in range(lo, hi):
+                nc.vector.tensor_scalar(
+                    out=y[n][:], in0=y[n][:], scalar1=neg_max[:, n : n + 1], scalar2=log_sum[:, n : n + 1],
+                    op0=ALU.add, op1=ALU.subtract,
+                )
+                store(n)
 
         with tc.manual_schedule():
             nc.vector.memset(b3_row[:], 0.0)
@@ -279,38 +286,38 @@ def tile_gcn_pc_kernel(tc, x_gc2, adj1, W3, b3, out):
             direct_sums(0)
             quantise(w_codes[TOP][:], w_scales[TOP][:], w_words[TOP][:])
             quantise(bot_codes[0][:], bot_scales[0][:], bot_words[0][:])
-            fold_rows(0)
 
             for j in range(PAIRS + LAG):
                 if j < PAIRS:
-                    adj_transposes(j)
+                    fold_rows(j)
                 if j >= LAG:
                     for n in tiles_of(j - LAG):
                         second_product(n)
                 if j < PAIRS:
+                    adj_transposes(j)
                     for n in tiles_of(j):
                         top_pass(n)
-                    if j + 1 < PAIRS:
-                        fold_rows(j + 1)
-                    adj_copies(j)
-                    folded_sums(j)
-                    if j + 1 < PAIRS:
-                        direct_sums(j + 1)
                 if j == 0:
                     bot_passes(2)
+                if j < PAIRS:
+                    folded_sums(j)
+                    adj_copies(j)
+                if j == 0:
                     bot_copies(2)
-                    quantise(bot_codes[1][:], bot_scales[1][:], bot_words[1][:])
-                if j == 1:
-                    quantise(bot_codes[2][:], bot_scales[2][:], bot_words[2][:])
+                if j + 1 < PAIRS:
+                    direct_sums(j + 1)
+                if j < GROUPS - 1:
+                    quantise(bot_codes[j + 1][:], bot_scales[j + 1][:], bot_words[j + 1][:])
                 if j >= LAG:
                     sums_and_maxima(j - LAG)
                     exponentials(j - LAG)
-                    if 2 * (j - LAG) + 2 == FIRST_LOG:
+                    if 2 * (j - LAG + 1) == FIRST_LOG:
                         logarithms(0, FIRST_LOG)
                 if j < PAIRS:
-                    quantise_adj(j)
                     scaled_top(j)
+                    quantise_adj(j)
                 if 2 * (j - LAG) == FIRST_LOG:
-                    finish(0, FIRST_LOG, False)
+                    finish_on_gpsimd(0, FINISHED_BY_GPSIMD)
+            finish_on_vector(FINISHED_BY_GPSIMD, FIRST_LOG)
             logarithms(FIRST_LOG, TILES)
-            finish(FIRST_LOG, TILES, True)
+            finish_on_vector(FIRST_LOG, TILES)

@@ -28,7 +28,9 @@ DEG_ON_SCALAR = (6, 8)
 BOT_COPY_ON_VECTOR = (0, 3)
 LAG = 2
 FIRST_LOG = 8
-FINISHED_BY_GPSIMD = 4
+EARLY = 4
+ROOT = 1024
+FINISHED_BY_GPSIMD = 6
 
 
 def tile_gcn_pc_kernel(tc, x_gc2, adj1, W3, b3, out):
@@ -70,6 +72,10 @@ def tile_gcn_pc_kernel(tc, x_gc2, adj1, W3, b3, out):
         b3_row = keep.tile([P, H], BF16, name="b3_row")
         b3_all = keep.tile([P, H], F32, name="b3_all")
         warm = keep.tile([P, 2], F32, name="warm")
+        exponent = keep.tile([P, EARLY], F32, name="exponent")
+        excess = keep.tile([P, EARLY], F32, name="excess")
+        series = keep.tile([P, EARLY], F32, name="series")
+        early_shift = keep.tile([P, EARLY], F32, name="early_shift")
 
         x_ps, bot_ps, adj_ps, adj_words, fold_ps, top_ps, ab_ps, b3_ps = {}, {}, {}, {}, {}, {}, {}, {}
 
@@ -232,13 +238,29 @@ def tile_gcn_pc_kernel(tc, x_gc2, adj1, W3, b3, out):
         def store(n):
             nc.sync.dma_start(out=out_v[:, n // 2, (n % 2) * H : (n % 2 + 1) * H], in_=y[n][:])
 
+        def finish_early():
+            cols = slice(0, EARLY)
+            nc.gpsimd.tensor_tensor(out=excess[:], in0=exp_sum[:, cols], in1=exponent[:], op=ALU.pow)
+            nc.gpsimd.tensor_scalar(out=excess[:], in0=excess[:], scalar1=1.0, scalar2=-1.0, op0=ALU.mult, op1=ALU.add)
+            nc.gpsimd.tensor_scalar(
+                out=series[:], in0=excess[:], scalar1=ROOT / 4, scalar2=-ROOT / 3, op0=ALU.mult, op1=ALU.add
+            )
+            for term in (ROOT / 2, -ROOT):
+                nc.gpsimd.tensor_tensor(out=series[:], in0=series[:], in1=excess[:], op=ALU.mult)
+                nc.gpsimd.tensor_scalar(out=series[:], in0=series[:], scalar1=1.0, scalar2=term, op0=ALU.mult, op1=ALU.add)
+            nc.gpsimd.tensor_tensor(out=series[:], in0=series[:], in1=excess[:], op=ALU.mult)
+            nc.gpsimd.tensor_tensor(out=early_shift[:], in0=series[:], in1=neg_max[:, cols], op=ALU.add)
+            for n in range(EARLY):
+                shift_on_gpsimd(n, early_shift[:, n : n + 1])
+
         def finish_on_gpsimd(lo, hi):
             nc.vector.tensor_tensor(out=shift[:, lo:hi], in0=neg_max[:, lo:hi], in1=log_sum[:, lo:hi], op=ALU.subtract)
             for n in range(lo, hi):
-                nc.gpsimd.tensor_scalar(
-                    out=y[n][:], in0=y[n][:], scalar1=1.0, scalar2=shift[:, n : n + 1], op0=ALU.mult, op1=ALU.add
-                )
-                store(n)
+                shift_on_gpsimd(n, shift[:, n : n + 1])
+
+        def shift_on_gpsimd(n, amount):
+            nc.gpsimd.tensor_scalar(out=y[n][:], in0=y[n][:], scalar1=1.0, scalar2=amount, op0=ALU.mult, op1=ALU.add)
+            store(n)
 
         def finish_on_vector(lo, hi):
             for n in range(lo, hi):
@@ -261,6 +283,7 @@ def tile_gcn_pc_kernel(tc, x_gc2, adj1, W3, b3, out):
             nc.vector.memset(warm[:], 0.0)
             nc.scalar.activation(out=warm[:, 1:2], in_=warm[:, 0:1], func=ACT.Exp)
             make_identity(nc, ident[:])
+            nc.gpsimd.memset(exponent[:], 1.0 / ROOT)
             nc.vector.memset(ones[:], 1.0)
             nc.vector.tensor_copy(out=ident_bf[:], in_=ident[:])
 
@@ -311,13 +334,15 @@ def tile_gcn_pc_kernel(tc, x_gc2, adj1, W3, b3, out):
                 if j >= LAG:
                     sums_and_maxima(j - LAG)
                     exponentials(j - LAG)
+                    if 2 * (j - LAG + 1) == EARLY:
+                        finish_early()
                     if 2 * (j - LAG + 1) == FIRST_LOG:
-                        logarithms(0, FIRST_LOG)
+                        logarithms(EARLY, FIRST_LOG)
                 if j < PAIRS:
                     scaled_top(j)
                     quantise_adj(j)
                 if 2 * (j - LAG) == FIRST_LOG:
-                    finish_on_gpsimd(0, FINISHED_BY_GPSIMD)
+                    finish_on_gpsimd(EARLY, FINISHED_BY_GPSIMD)
             finish_on_vector(FINISHED_BY_GPSIMD, FIRST_LOG)
             logarithms(FIRST_LOG, TILES)
             finish_on_vector(FIRST_LOG, TILES)

@@ -24,12 +24,13 @@ TOP = 0
 BOT = 1
 
 DEG_ON_TENSOR = (1, 3, 5, 7, 9, 10, 11)
-DEG_ON_SCALAR = (6, 8)
+DEG_ON_SCALAR = (4, 6, 8)
 BOT_COPY_ON_VECTOR = (0, 3)
 LAG = 2
 FIRST_LOG = 8
 EARLY = 4
 ROOT = 1024
+LATE = (8, 10)
 FINISHED_BY_GPSIMD = 6
 
 
@@ -72,6 +73,7 @@ def tile_gcn_pc_kernel(tc, x_gc2, adj1, W3, b3, out):
         b3_row = keep.tile([P, H], BF16, name="b3_row")
         b3_all = keep.tile([P, H], F32, name="b3_all")
         warm = keep.tile([P, 2], F32, name="warm")
+        late_root, late_excess, late_series = [keep.tile([P, 2], F32, name="late%d" % i) for i in range(3)]
         exponent = keep.tile([P, EARLY], F32, name="exponent")
         excess = keep.tile([P, EARLY], F32, name="excess")
         series = keep.tile([P, EARLY], F32, name="series")
@@ -235,6 +237,27 @@ def tile_gcn_pc_kernel(tc, x_gc2, adj1, W3, b3, out):
         def logarithms(lo, hi):
             nc.scalar.activation(out=log_sum[:, lo:hi], in_=exp_sum[:, lo:hi], func=ACT.Ln)
 
+        def late_roots():
+            lo, hi = LATE
+            nc.gpsimd.tensor_tensor(out=late_root[:], in0=exp_sum[:, lo:hi], in1=exponent[:, 0:2], op=ALU.pow)
+
+        def late_logs():
+            nc.vector.tensor_scalar(
+                out=late_excess[:], in0=late_root[:], scalar1=1.0, scalar2=-1.0, op0=ALU.mult, op1=ALU.add
+            )
+            between = list(range(FINISHED_BY_GPSIMD, FIRST_LOG))
+            for in_, number in ((late_excess, -4 / 3), (late_series, 2.0), (late_series, -4.0)):
+                if between:
+                    finish_on_vector(between[0], between[0] + 1)
+                    between = between[1:]
+                nc.vector.scalar_tensor_tensor(
+                    out=late_series[:], in0=in_[:], scalar=number, in1=late_excess[:], op0=ALU.add, op1=ALU.mult
+                )
+            lo, hi = LATE
+            nc.vector.tensor_scalar(
+                out=log_sum[:, lo:hi], in0=late_series[:], scalar1=-ROOT / 4, scalar2=0.0, op0=ALU.mult, op1=ALU.add
+            )
+
         def store(n):
             nc.sync.dma_start(out=out_v[:, n // 2, (n % 2) * H : (n % 2 + 1) * H], in_=y[n][:])
 
@@ -272,11 +295,11 @@ def tile_gcn_pc_kernel(tc, x_gc2, adj1, W3, b3, out):
 
         with tc.manual_schedule():
             nc.vector.memset(b3_row[:], 0.0)
-            nc.scalar.dma_start(out=b3_row[0:1, :], in_=b3.unsqueeze(0))
             for g in range(GROUPS):
                 nc.sync.dma_start(out=x_rows[g][:].rearrange("m (a f) -> m a f", a=2), in_=x_v[:, 2 * g : 2 * g + 2, :])
                 if g == 0:
                     nc.sync.dma_start(out=w_rows[BOT][:].rearrange("q (u f) -> q u f", u=2), in_=w_v[:, BOT])
+                    nc.sync.dma_start(out=b3_row[0:1, :], in_=b3.unsqueeze(0))
             nc.sync.dma_start(out=w_rows[TOP][:].rearrange("q (u f) -> q u f", u=2), in_=w_v[:, TOP])
             for a in range(PAIRS):
                 nc.sync.dma_start(out=adj_rows[a][:], in_=adj_v[:, a, :])
@@ -311,13 +334,14 @@ def tile_gcn_pc_kernel(tc, x_gc2, adj1, W3, b3, out):
             quantise(bot_codes[0][:], bot_scales[0][:], bot_words[0][:])
 
             for j in range(PAIRS + LAG):
-                if j < PAIRS:
-                    fold_rows(j)
                 if j >= LAG:
                     for n in tiles_of(j - LAG):
                         second_product(n)
                 if j < PAIRS:
+                    fold_rows(j)
+                if j < PAIRS:
                     adj_transposes(j)
+                if j < PAIRS:
                     for n in tiles_of(j):
                         top_pass(n)
                 if j == 0:
@@ -343,6 +367,8 @@ def tile_gcn_pc_kernel(tc, x_gc2, adj1, W3, b3, out):
                     quantise_adj(j)
                 if 2 * (j - LAG) == FIRST_LOG:
                     finish_on_gpsimd(EARLY, FINISHED_BY_GPSIMD)
-            finish_on_vector(FINISHED_BY_GPSIMD, FIRST_LOG)
-            logarithms(FIRST_LOG, TILES)
-            finish_on_vector(FIRST_LOG, TILES)
+                    late_roots()
+            logarithms(TILES - 2, TILES)
+            late_logs()
+            finish_on_vector(*LATE)
+            finish_on_vector(TILES - 2, TILES)

@@ -26,6 +26,7 @@ BOT = 1
 DEG_ON_TENSOR = (1, 3, 5, 7, 9, 10, 11)
 DEG_ON_SCALAR = (4, 6, 8)
 BOT_COPY_ON_VECTOR = (0, 3)
+FIRST_OF_CALL = (0, 2)
 LAG = 2
 FIRST_LOG = 8
 EARLY = 4
@@ -38,7 +39,7 @@ def tile_gcn_pc_kernel(tc, x_gc2, adj1, W3, b3, out):
     nc = tc.nc
     with ExitStack() as ctx:
         keep = ctx.enter_context(tc.tile_pool(name="keep", bufs=1))
-        regrouped = ctx.enter_context(tc.tile_pool(name="regrouped", bufs=9))
+        regrouped = ctx.enter_context(tc.tile_pool(name="regrouped", bufs=3))
         unread = ctx.enter_context(tc.tile_pool(name="unread", bufs=2))
         psum = ctx.enter_context(tc.psum_pool(name="psum", bufs=8))
 
@@ -77,7 +78,8 @@ def tile_gcn_pc_kernel(tc, x_gc2, adj1, W3, b3, out):
         exponent = keep.tile([P, EARLY], F32, name="exponent")
         excess = keep.tile([P, EARLY], F32, name="excess")
         series = keep.tile([P, EARLY], F32, name="series")
-        early_shift = keep.tile([P, EARLY], F32, name="early_shift")
+        early_shift = keep.tile([P, 2], F32, name="early_shift")
+        held_shift = keep.tile([P, EARLY - 2], F32, name="held_shift")
 
         x_ps, bot_ps, adj_ps, adj_words, fold_ps, top_ps, ab_ps, b3_ps = {}, {}, {}, {}, {}, {}, {}, {}
 
@@ -167,9 +169,13 @@ def tile_gcn_pc_kernel(tc, x_gc2, adj1, W3, b3, out):
 
         def adj_copies(a):
             for g in range(GROUPS):
-                adj_words[a, g] = regrouped.tile([P, 2 * H], BF16, name="adj_words", align_bytes=64)
+                if g in FIRST_OF_CALL:
+                    width = 2 * H * (2 if g == 0 else 1)
+                    words = regrouped.tile([P, width], BF16, name="adj_words%d" % g, align_bytes=64)
+                    adj_words[a, g] = words
+                half = words[:, 2 * H * (g % 2) : 2 * H * (g % 2 + 1)]
                 nc.scalar.copy(
-                    out=adj_words[a, g][:].bitcast(F32).rearrange("q (e i u) -> q e i u", e=2, i=P, u=2),
+                    out=half.bitcast(F32).rearrange("q (e i u) -> q e i u", e=2, i=P, u=2),
                     in_=adj_ps[a, g][:].rearrange("q (e u i) -> q e i u", e=2, u=2, i=P),
                 )
 
@@ -210,8 +216,7 @@ def tile_gcn_pc_kernel(tc, x_gc2, adj1, W3, b3, out):
             nc.vector.quantize_mx(out=codes.bitcast(FP8X4), scales=scales, in_=words)
 
         def quantise_adj(a):
-            for g in range(GROUPS):
-                cols = slice(g * 2 * P, (g + 1) * 2 * P)
+            for g, cols in zip(FIRST_OF_CALL, (slice(0, 4 * P), slice(4 * P, 6 * P))):
                 quantise(adj_codes[a][:, cols], adj_scales[a][:, cols], adj_words[a, g][:])
 
         def scaled_top(a):
@@ -242,14 +247,12 @@ def tile_gcn_pc_kernel(tc, x_gc2, adj1, W3, b3, out):
             nc.gpsimd.tensor_tensor(out=late_root[:], in0=exp_sum[:, lo:hi], in1=exponent[:, 0:2], op=ALU.pow)
 
         def late_logs():
+            finish_on_vector(FINISHED_BY_GPSIMD, FIRST_LOG - 1)
             nc.vector.tensor_scalar(
                 out=late_excess[:], in0=late_root[:], scalar1=1.0, scalar2=-1.0, op0=ALU.mult, op1=ALU.add
             )
-            between = list(range(FINISHED_BY_GPSIMD, FIRST_LOG))
+            finish_on_vector(FIRST_LOG - 1, FIRST_LOG)
             for in_, number in ((late_excess, -4 / 3), (late_series, 2.0), (late_series, -4.0)):
-                if between:
-                    finish_on_vector(between[0], between[0] + 1)
-                    between = between[1:]
                 nc.vector.scalar_tensor_tensor(
                     out=late_series[:], in0=in_[:], scalar=number, in1=late_excess[:], op0=ALU.add, op1=ALU.mult
                 )
@@ -272,9 +275,14 @@ def tile_gcn_pc_kernel(tc, x_gc2, adj1, W3, b3, out):
                 nc.gpsimd.tensor_tensor(out=series[:], in0=series[:], in1=excess[:], op=ALU.mult)
                 nc.gpsimd.tensor_scalar(out=series[:], in0=series[:], scalar1=1.0, scalar2=term, op0=ALU.mult, op1=ALU.add)
             nc.gpsimd.tensor_tensor(out=series[:], in0=series[:], in1=excess[:], op=ALU.mult)
-            nc.gpsimd.tensor_tensor(out=early_shift[:], in0=series[:], in1=neg_max[:, cols], op=ALU.add)
-            for n in range(EARLY):
+            nc.gpsimd.tensor_tensor(out=early_shift[:], in0=series[:, 0:2], in1=neg_max[:, 0:2], op=ALU.add)
+            for n in range(2):
                 shift_on_gpsimd(n, early_shift[:, n : n + 1])
+
+        def finish_held():
+            nc.vector.tensor_tensor(out=held_shift[:], in0=series[:, 2:EARLY], in1=neg_max[:, 2:EARLY], op=ALU.add)
+            for n in range(2, EARLY):
+                shift_on_gpsimd(n, held_shift[:, n - 2 : n - 1])
 
         def finish_on_gpsimd(lo, hi):
             nc.vector.tensor_tensor(out=shift[:, lo:hi], in0=neg_max[:, lo:hi], in1=log_sum[:, lo:hi], op=ALU.subtract)
@@ -365,6 +373,8 @@ def tile_gcn_pc_kernel(tc, x_gc2, adj1, W3, b3, out):
                 if j < PAIRS:
                     scaled_top(j)
                     quantise_adj(j)
+                if j == PAIRS - 1:
+                    finish_held()
                 if 2 * (j - LAG) == FIRST_LOG:
                     finish_on_gpsimd(EARLY, FINISHED_BY_GPSIMD)
                     late_roots()

from contextlib import ExitStack

import concourse.mybir as mybir
from concourse.masks import make_identity

FLOPS = 2 * 1536 * 512 * 512 * 2 + 2 * 1536 * 1536 * 512

F32 = mybir.dt.float32
BF16 = mybir.dt.bfloat16
U32 = mybir.dt.uint32
U8 = mybir.dt.uint8
FP8X4 = mybir.dt.float8_e4m3fn_x4
ALU = mybir.AluOpType
ACT = mybir.ActivationFunctionType
AX = mybir.AxisListType

P = 128
H = 512
NODES = 1536
GROUPS = NODES // H
PAIRS = NODES // (2 * P)
TILES = 2 * PAIRS
TOP = 0
BOT = 1

DEG_ON_TENSOR = (1, 3, 5, 7, 9, 10, 11)
DEG_ON_SCALAR = (4, 6, 8)
BOT_COPY_ON_VECTOR = (0, 3)
FIRST_OF_CALL = (0, 2)
LAG = 2
FIRST_LOG = 8
EARLY = 4
ROOT = 1024
LATE = (8, 10)
FINISHED_BY_GPSIMD = 6


def tile_gcn_pc_kernel(tc, x_gc2, adj1, W3, b3, out):
    nc = tc.nc
    with ExitStack() as ctx:
        keep = ctx.enter_context(tc.tile_pool(name="keep", bufs=1))
        regrouped = ctx.enter_context(tc.tile_pool(name="regrouped", bufs=3))
        unread = ctx.enter_context(tc.tile_pool(name="unread", bufs=2))
        psum = ctx.enter_context(tc.psum_pool(name="psum", bufs=8))

        x_v = x_gc2.rearrange("(a m e) k -> m a (e k)", a=PAIRS, m=P, e=2)
        adj_v = adj1.rearrange("(a m e) j -> m a (e j)", a=PAIRS, m=P, e=2)
        out_v = out.rearrange("(a m e) c -> m a (e c)", a=PAIRS, m=P, e=2)
        w_v = W3.rearrange("(w u q e) c -> q w u (e c)", w=2, u=2, q=P, e=2)

        w_rows = [keep.tile([P, 4 * H], BF16, name="w_rows%d" % w) for w in range(2)]
        w_words = [keep.tile([P, 4 * H], BF16, name="w_words%d" % w, align_bytes=64) for w in range(2)]
        w_codes = [keep.tile([P, H], U32, name="w_codes%d" % w, align_bytes=64) for w in range(2)]
        w_scales = [keep.tile([P, H], U8, name="w_scales%d" % w, align_bytes=64) for w in range(2)]
        x_rows = [keep.tile([P, 4 * H], BF16, name="x_rows%d" % g) for g in range(GROUPS)]
        x_words = [keep.tile([P, 4 * H], BF16, name="x_words%d" % g, align_bytes=64) for g in range(GROUPS)]
        x_codes = [keep.tile([P, H], U32, name="x_codes%d" % g, align_bytes=64) for g in range(GROUPS)]
        x_scales = [keep.tile([P, H], U8, name="x_scales%d" % g, align_bytes=64) for g in range(GROUPS)]
        bot_words = [keep.tile([P, 4 * H], BF16, name="bot_words%d" % g, align_bytes=64) for g in range(GROUPS)]
        bot_codes = [keep.tile([P, H], U32, name="bot_codes%d" % g, align_bytes=64) for g in range(GROUPS)]
        bot_scales = [keep.tile([P, H], U8, name="bot_scales%d" % g, align_bytes=64) for g in range(GROUPS)]
        adj_rows = [keep.tile([P, 2 * NODES], BF16, name="adj_rows%d" % a) for a in range(PAIRS)]
        adj_codes = [keep.tile([P, GROUPS * 2 * P], U32, name="adj_codes%d" % a, align_bytes=64) for a in range(PAIRS)]
        adj_scales = [keep.tile([P, GROUPS * 2 * P], U8, name="adj_scales%d" % a, align_bytes=64) for a in range(PAIRS)]
        y = [keep.tile([P, H], F32, name="y%d" % n) for n in range(TILES)]
        deg = [keep.tile([P, 1], F32, name="deg%d" % n) for n in range(TILES)]
        neg_max = keep.tile([P, TILES], F32, name="neg_max")
        exp_sum = keep.tile([P, TILES], F32, name="exp_sum")
        log_sum = keep.tile([P, TILES], F32, name="log_sum")
        shift = keep.tile([P, TILES], F32, name="shift")
        ident = keep.tile([P, P], F32, name="ident")
        ident_bf = keep.tile([P, P], BF16, name="ident_bf")
        ones = keep.tile([P, P], BF16, name="ones")
        b3_row = keep.tile([P, H], BF16, name="b3_row")
        b3_all = keep.tile([P, H], F32, name="b3_all")
        warm = keep.tile([P, 2], F32, name="warm")
        late_root, late_excess, late_series = [keep.tile([P, 2], F32, name="late%d" % i) for i in range(3)]
        exponent = keep.tile([P, EARLY], F32, name="exponent")
        excess = keep.tile([P, EARLY], F32, name="excess")
        series = keep.tile([P, EARLY], F32, name="series")
        early_shift = keep.tile([P, 2], F32, name="early_shift")
        held_shift = keep.tile([P, EARLY - 2], F32, name="held_shift")

        x_ps, bot_ps, adj_ps, adj_words, fold_ps, top_ps, ab_ps, b3_ps = {}, {}, {}, {}, {}, {}, {}, {}

        def bank():
            return psum.tile([P, H], F32, name="bank")

        def tiles_of(a):
            return (2 * a, 2 * a + 1)

        def rows_of(n):
            return adj_rows[n // 2][:, (n % 2) * NODES : (n % 2 + 1) * NODES]

        def transpose_words(dst, words, columns):
            for i, col in enumerate(columns):
                nc.tensor.transpose(dst[:, i * P : (i + 1) * P], words[:, col : col + P], ident[:])

        def x_transposes(g):
            for b in range(2):
                x_ps[g, b] = bank()
                transpose_words(x_ps[g, b], x_rows[g][:].bitcast(F32), [(4 * b + i) * P for i in range(4)])

        def adj_transposes(a):
            for g in range(GROUPS):
                adj_ps[a, g] = bank()
                transpose_words(
                    adj_ps[a, g], adj_rows[a][:].bitcast(F32), [e * (NODES // 2) + (2 * g + u) * P for e in range(2) for u in range(2)]
                )

        def mx_pass(dst, lhs_codes, lhs_scales, lhs_cols, rhs_codes, rhs_scales, rhs_cols, start, stop):
            nc.tensor.matmul_mx(
                out=dst,
                lhsT=lhs_codes[:, lhs_cols].bitcast(FP8X4),
                lhsT_scale=lhs_scales[:, lhs_cols],
                rhs=rhs_codes[:, rhs_cols].bitcast(FP8X4),
                rhs_scale=rhs_scales[:, rhs_cols],
                start=start,
                stop=stop,
            )

        def bot_passes(g):
            for c in range(4):
                bot_ps[g, c] = bank()
                for t in range(4):
                    mx_pass(
                        bot_ps[g, c][:, t * P : (t + 1) * P],
                        x_codes[g], x_scales[g], slice(t * P, (t + 1) * P),
                        w_codes[BOT], w_scales[BOT], slice(c * P, (c + 1) * P),
                        True, True,
                    )

        def top_pass(n):
            top_ps[n] = bank()
            mx_pass(
                top_ps[n][:],
                x_codes[n // 4], x_scales[n // 4], slice((n % 4) * P, (n % 4 + 1) * P),
                w_codes[TOP], w_scales[TOP], slice(0, H),
                True, True,
            )

        def second_product(n):
            ab_ps[n] = bank()
            for g in range(GROUPS):
                col = (2 * g + n % 2) * P
                mx_pass(
                    ab_ps[n][:],
                    adj_codes[n // 2], adj_scales[n // 2], slice(col, col + P),
                    bot_codes[g], bot_scales[g], slice(0, H),
                    g == 0, g == GROUPS - 1,
                )

        def fold_rows(a):
            for n in tiles_of(a):
                if n in DEG_ON_TENSOR:
                    fold_ps[n] = bank()
                    for r in range(NODES // P):
                        nc.tensor.matmul(
                            out=fold_ps[n][:, 0:P], lhsT=ident_bf[:], rhs=rows_of(n)[:, r * P : (r + 1) * P],
                            start=(r == 0), stop=(r == NODES // P - 1),
                        )

        def x_copies(g):
            for b in range(2):
                nc.scalar.copy(
                    out=x_words[g][:].bitcast(F32)[:, b * H : (b + 1) * H].rearrange("q (n r u) -> q n r u", n=2, r=P, u=2),
                    in_=x_ps[g, b][:].rearrange("q (n u r) -> q n r u", n=2, u=2, r=P),
                )

        def adj_copies(a):
            for g in range(GROUPS):
                if g in FIRST_OF_CALL:
                    width = 2 * H * (2 if g == 0 else 1)
                    words = regrouped.tile([P, width], BF16, name="adj_words%d" % g, align_bytes=64)
                    adj_words[a, g] = words
                half = words[:, 2 * H * (g % 2) : 2 * H * (g % 2 + 1)]
                nc.scalar.copy(
                    out=half.bitcast(F32).rearrange("q (e i u) -> q e i u", e=2, i=P, u=2),
                    in_=adj_ps[a, g][:].rearrange("q (e u i) -> q e i u", e=2, u=2, i=P),
                )

        def bot_copies(g):
            for c in range(4):
                dst = bot_words[g][:, c * H : (c + 1) * H].rearrange("m (c t) -> m c t", c=P, t=4)
                src = bot_ps[g, c][:].rearrange("m (t c) -> m c t", t=4, c=P)
                if (g, c) == BOT_COPY_ON_VECTOR:
                    nc.vector.tensor_copy(out=dst, in_=src)
                else:
                    nc.scalar.copy(out=dst, in_=src)

        def folded_sums(a):
            for n in tiles_of(a):
                if n in DEG_ON_TENSOR:
                    copied = unread.tile([P, P], F32, name="copied")
                    nc.scalar.activation(out=copied[:], in_=fold_ps[n][:, 0:P], func=ACT.Copy, accum_out=deg[n][:])

        def direct_sums(a):
            for n in tiles_of(a):
                if n not in DEG_ON_TENSOR:
                    copied = unread.tile([P, NODES], BF16, name="rows_copied")
                    if n in DEG_ON_SCALAR:
                        nc.scalar.activation(out=copied[:], in_=rows_of(n), func=ACT.Copy, accum_out=deg[n][:])
                    else:
                        nc.vector.tensor_scalar(
                            out=copied[:], in0=rows_of(n), scalar1=1.0, scalar2=None, op0=ALU.mult, op1=ALU.add,
                            accum_out=deg[n][:],
                        )

        def regroup_w(w):
            nc.vector.tensor_copy(
                out=w_words[w][:].rearrange("p (c i t) -> p c t i", c=P, i=4, t=4),
                in_=w_rows[w][:].rearrange("p (t c i) -> p c t i", t=4, c=P, i=4),
            )

        def quantise(codes, scales, words):
            nc.vector.quantize_mx(out=codes.bitcast(FP8X4), scales=scales, in_=words)

        def quantise_adj(a):
            for g, cols in zip(FIRST_OF_CALL, (slice(0, 4 * P), slice(4 * P, 6 * P))):
                quantise(adj_codes[a][:, cols], adj_scales[a][:, cols], adj_words[a, g][:])

        def scaled_top(a):
            for n in tiles_of(a):
                nc.vector.scalar_tensor_tensor(
                    out=y[n][:], in0=top_ps[n][:], scalar=deg[n][:], in1=b3_all[:], op0=ALU.mult, op1=ALU.add
                )

        def sums_and_maxima(a):
            for n in tiles_of(a):
                nc.vector.tensor_tensor(out=y[n][:], in0=ab_ps[n][:], in1=y[n][:], op=ALU.add)
            for n in tiles_of(a):
                nc.vector.tensor_reduce(out=neg_max[:, n : n + 1], in_=y[n][:], axis=AX.X, op=ALU.max, negate=True)

        def exponentials(a):
            for n in tiles_of(a):
                powers = unread.tile([P, H], BF16, name="powers")
                nc.scalar.activation(
                    out=powers[:], in_=y[n][:], func=ACT.Exp, bias=neg_max[:, n : n + 1], scale=1.0,
                    accum_out=exp_sum[:, n : n + 1],
                )

        def logarithms(lo, hi):
            nc.scalar.activation(out=log_sum[:, lo:hi], in_=exp_sum[:, lo:hi], func=ACT.Ln)

        def late_roots():
            lo, hi = LATE
            nc.gpsimd.tensor_tensor(out=late_root[:], in0=exp_sum[:, lo:hi], in1=exponent[:, 0:2], op=ALU.pow)

        def late_logs():
            finish_on_vector(FINISHED_BY_GPSIMD, FIRST_LOG - 1)
            nc.vector.tensor_scalar(
                out=late_excess[:], in0=late_root[:], scalar1=1.0, scalar2=-1.0, op0=ALU.mult, op1=ALU.add
            )
            finish_on_vector(FIRST_LOG - 1, FIRST_LOG)
            for in_, number in ((late_excess, -4 / 3), (late_series, 2.0), (late_series, -4.0)):
                nc.vector.scalar_tensor_tensor(
                    out=late_series[:], in0=in_[:], scalar=number, in1=late_excess[:], op0=ALU.add, op1=ALU.mult
                )
            lo, hi = LATE
            nc.vector.tensor_scalar(
                out=log_sum[:, lo:hi], in0=late_series[:], scalar1=-ROOT / 4, scalar2=0.0, op0=ALU.mult, op1=ALU.add
            )

        def store(n):
            nc.sync.dma_start(out=out_v[:, n // 2, (n % 2) * H : (n % 2 + 1) * H], in_=y[n][:])

        def finish_early():
            cols = slice(0, EARLY)
            nc.gpsimd.tensor_tensor(out=excess[:], in0=exp_sum[:, cols], in1=exponent[:], op=ALU.pow)
            nc.gpsimd.tensor_scalar(out=excess[:], in0=excess[:], scalar1=1.0, scalar2=-1.0, op0=ALU.mult, op1=ALU.add)
            nc.gpsimd.tensor_scalar(
                out=series[:], in0=excess[:], scalar1=ROOT / 4, scalar2=-ROOT / 3, op0=ALU.mult, op1=ALU.add
            )
            for term in (ROOT / 2, -ROOT):
                nc.gpsimd.tensor_tensor(out=series[:], in0=series[:], in1=excess[:], op=ALU.mult)
                nc.gpsimd.tensor_scalar(out=series[:], in0=series[:], scalar1=1.0, scalar2=term, op0=ALU.mult, op1=ALU.add)
            nc.gpsimd.tensor_tensor(out=series[:], in0=series[:], in1=excess[:], op=ALU.mult)
            nc.gpsimd.tensor_tensor(out=early_shift[:], in0=series[:, 0:2], in1=neg_max[:, 0:2], op=ALU.add)
            for n in range(2):
                shift_on_gpsimd(n, early_shift[:, n : n + 1])

        def finish_held():
            nc.vector.tensor_tensor(out=held_shift[:], in0=series[:, 2:EARLY], in1=neg_max[:, 2:EARLY], op=ALU.add)
            for n in range(2, EARLY):
                shift_on_gpsimd(n, held_shift[:, n - 2 : n - 1])

        def finish_on_gpsimd(lo, hi):
            nc.vector.tensor_tensor(out=shift[:, lo:hi], in0=neg_max[:, lo:hi], in1=log_sum[:, lo:hi], op=ALU.subtract)
            for n in range(lo, hi):
                shift_on_gpsimd(n, shift[:, n : n + 1])

        def shift_on_gpsimd(n, amount):
            nc.gpsimd.tensor_scalar(out=y[n][:], in0=y[n][:], scalar1=1.0, scalar2=amount, op0=ALU.mult, op1=ALU.add)
            store(n)

        def finish_on_vector(lo, hi):
            for n in range(lo, hi):
                nc.vector.tensor_scalar(
                    out=y[n][:], in0=y[n][:], scalar1=neg_max[:, n : n + 1], scalar2=log_sum[:, n : n + 1],
                    op0=ALU.add, op1=ALU.subtract,
                )
                store(n)

        with tc.manual_schedule():
            nc.vector.memset(b3_row[:], 0.0)
            for g in range(GROUPS):
                nc.sync.dma_start(out=x_rows[g][:].rearrange("m (a f) -> m a f", a=2), in_=x_v[:, 2 * g : 2 * g + 2, :])
                if g == 0:
                    nc.sync.dma_start(out=w_rows[BOT][:].rearrange("q (u f) -> q u f", u=2), in_=w_v[:, BOT])
                    nc.sync.dma_start(out=b3_row[0:1, :], in_=b3.unsqueeze(0))
            nc.sync.dma_start(out=w_rows[TOP][:].rearrange("q (u f) -> q u f", u=2), in_=w_v[:, TOP])
            for a in range(PAIRS):
                nc.sync.dma_start(out=adj_rows[a][:], in_=adj_v[:, a, :])
            nc.vector.memset(warm[:], 0.0)
            nc.scalar.activation(out=warm[:, 1:2], in_=warm[:, 0:1], func=ACT.Exp)
            make_identity(nc, ident[:])
            nc.gpsimd.memset(exponent[:], 1.0 / ROOT)
            nc.vector.memset(ones[:], 1.0)
            nc.vector.tensor_copy(out=ident_bf[:], in_=ident[:])

            x_transposes(0)
            x_copies(0)
            regroup_w(BOT)
            b3_ps[0] = bank()
            nc.tensor.matmul(out=b3_ps[0][:], lhsT=ones[:], rhs=b3_row[:], start=True, stop=True)
            nc.scalar.copy(out=b3_all[:], in_=b3_ps[0][:])
            quantise(x_codes[0][:], x_scales[0][:], x_words[0][:])
            x_transposes(1)
            x_copies(1)
            quantise(w_codes[BOT][:], w_scales[BOT][:], w_words[BOT][:])
            quantise(x_codes[1][:], x_scales[1][:], x_words[1][:])
            x_transposes(2)
            x_copies(2)
            regroup_w(TOP)
            quantise(x_codes[2][:], x_scales[2][:], x_words[2][:])
            bot_passes(0)
            bot_copies(0)
            bot_passes(1)
            bot_copies(1)
            direct_sums(0)
            quantise(w_codes[TOP][:], w_scales[TOP][:], w_words[TOP][:])
            quantise(bot_codes[0][:], bot_scales[0][:], bot_words[0][:])

            for j in range(PAIRS + LAG):
                if j >= LAG:
                    for n in tiles_of(j - LAG):
                        second_product(n)
                if j < PAIRS:
                    fold_rows(j)
                if j < PAIRS:
                    adj_transposes(j)
                if j < PAIRS:
                    for n in tiles_of(j):
                        top_pass(n)
                if j == 0:
                    bot_passes(2)
                if j < PAIRS:
                    folded_sums(j)
                    adj_copies(j)
                if j == 0:
                    bot_copies(2)
                if j + 1 < PAIRS:
                    direct_sums(j + 1)
                if j < GROUPS - 1:
                    quantise(bot_codes[j + 1][:], bot_scales[j + 1][:], bot_words[j + 1][:])
                if j >= LAG:
                    sums_and_maxima(j - LAG)
                    exponentials(j - LAG)
                    if 2 * (j - LAG + 1) == EARLY:
                        finish_early()
                    if 2 * (j - LAG + 1) == FIRST_LOG:
                        logarithms(EARLY, FIRST_LOG)
                if j < PAIRS:
                    scaled_top(j)
                    quantise_adj(j)
                if j == PAIRS - 1:
                    finish_held()
                if 2 * (j - LAG) == FIRST_LOG:
                    finish_on_gpsimd(EARLY, FINISHED_BY_GPSIMD)
                    late_roots()
            logarithms(TILES - 2, TILES)
            late_logs()
            finish_on_vector(*LATE)
            finish_on_vector(TILES - 2, TILES)
